import numpy as np
import ml_dtypes


def mxq(x, axis, fmt="e4m3"):
    dtype, down = {"e4m3": (ml_dtypes.float8_e4m3fn, 7), "e5m2": (ml_dtypes.float8_e5m2, 14)}[fmt]
    v = np.moveaxis(np.asarray(x, np.float32).astype(ml_dtypes.bfloat16).astype(np.float64), axis, -1)
    blocks = v.reshape(v.shape[:-1] + (-1, 32))
    amax = np.abs(blocks).max(-1, keepdims=True)
    byte = np.maximum(np.where(amax > 0, np.frexp(amax)[1] - 1 + 127, 0) - down, 1)
    scale = np.exp2(byte - 127.0)
    codes = (blocks / scale).astype(np.float32).astype(dtype).astype(np.float64)
    return np.moveaxis((codes * scale).reshape(v.shape), -1, axis)


WIDE = False


def mx_kscale(k):
    if not WIDE:
        return np.ones(k)
    levels = np.array([10, -10, 5, -5, 0])
    if k % 512:
        return np.exp2(np.random.permutation(np.resize(levels, k // 32))).repeat(32)
    a = np.empty((k // 512, 16))
    for p in range(k // 512):
        a[p, :8] = np.random.permutation(np.resize(levels, 8))
        for g in range(8):
            far = levels[np.abs(levels - a[p, g]) >= 10]
            a[p, g + 8] = far[np.random.randint(len(far))]
    return np.exp2(a.ravel()).repeat(32)


BF16 = ml_dtypes.bfloat16


def bf(x):
    return np.asarray(x, np.float32).astype(BF16)


def f64(x):
    return np.asarray(x).astype(np.float64)


B, F, D, HALF, OUT = 512, 4, 32, 128, 128
CL = HALF + HALF
FINAL = HALF + HALF + CL


def cin_layer(x0, h, w, b):
    n, nf, nd = x0.shape
    ng, no = h.shape[1], w.shape[0]
    p = (x0.transpose(0, 2, 1)[:, :, :, None] * h.transpose(0, 2, 1)[:, :, None, :]).reshape(n * nd, nf * ng)
    z = (mxq(p, 1, "e4m3") @ mxq(w.reshape(no, nf * ng).T, 0, "e4m3")) + b
    return np.maximum(z, 0.0).reshape(n, nd, no).transpose(0, 2, 1)


def draw0():
    s = mx_kscale(F * HALF).reshape(F, HALF)
    u, t = s[:, 0], s[0]
    v = mx_kscale(FINAL)
    return {"x": bf(np.random.standard_normal((B, F, D)) * u[None, :, None]),
            "x1": bf(np.maximum(np.random.standard_normal((B, HALF, D)), 0.0) * 0.75 * v[:HALF][None, :, None]),
            "x2": bf(np.maximum(np.random.standard_normal((B, HALF, D)), 0.0) * 0.75 * v[HALF:CL][None, :, None]),
            "h2": bf(np.maximum(np.random.standard_normal((B, HALF, D)), 0.0) * 0.75 * t[None, :, None]),
            "w3": bf(np.random.standard_normal((CL, F, HALF)) * 1.25 / np.sqrt(F * HALF) * v[CL:][:, None, None] / (u[:, None] * t[None, :])),
            "b3": bf(np.random.standard_normal(CL) * 0.3 * v[CL:]),
            "out_w": bf(np.random.standard_normal((FINAL, OUT)) * 6.0 / (D * np.sqrt(FINAL)) / v[:, None]),
            "out_b": bf(np.random.standard_normal(OUT) * 0.5)}


def core(x, x1, x2, h2, w3, b3, out_w, out_b):
    y3 = cin_layer(f64(x), f64(h2), f64(w3), f64(b3))
    pooled = np.concatenate([f64(x1), f64(x2), y3], axis=1).sum(axis=2)
    return (mxq(pooled, 1, "e4m3") @ mxq(f64(out_w), 0, "e4m3")) + f64(out_b)


def e4m3fn_bytes(y):
    return np.clip(np.asarray(y, np.float64), -448.0, 448.0).astype(np.float32).astype(ml_dtypes.float8_e4m3fn).view(np.uint8)


def e4m3fn_values(b):
    return np.asarray(b, np.uint8).view(ml_dtypes.float8_e4m3fn).astype(np.float64)


def setup_inputs():
    d = draw0()
    x0 = np.asarray(d['out_w']).astype(np.float64)
    s = (np.max(np.abs(x0), axis=(1,), keepdims=True) / 448.0).astype(np.float32)
    out = {}
    for k, v in d.items():
        if k == 'out_w':
            out['out_w_bytes'] = e4m3fn_bytes(x0 / s.astype(np.float64))
            out['out_w_scale'] = s
        else:
            out[k] = v
    return out


def reference(x, x1, x2, h2, w3, b3, out_w_bytes, out_w_scale, out_b):
    return core(x, x1, x2, h2, w3, b3, e4m3fn_values(out_w_bytes) * out_w_scale.astype(np.float64), out_b)

@@ -1,0 +1,349 @@
+from contextlib import ExitStack
+
+import concourse.mybir as mybir
+from concourse.masks import make_identity
+
+F32 = mybir.dt.float32
+BF16 = mybir.dt.bfloat16
+U32 = mybir.dt.uint32
+U8 = mybir.dt.uint8
+FP8 = mybir.dt.float8_e4m3fn
+FP8X4 = mybir.dt.float8_e4m3fn_x4
+ALU = mybir.AluOpType
+ACT = mybir.ActivationFunctionType
+AX = mybir.AxisListType
+
+B, F, D, G, OC = 512, 4, 32, 128, 256
+FINAL, NOUT = 512, 128
+P = 128
+FLOPS = 2 * B * D * F * G * OC + 2 * B * FINAL * NOUT
+
+NT = B // P
+CD = 4
+CHUNKS = NT * D // CD
+PER_NT = D // CD
+GD = 8
+GROUPS = CHUNKS // 2
+PLAIN_D = 12
+PAIRS = (D - PLAIN_D) // 2
+
+
+def tile_cin_pb_t_kernel(tc, x, x1, x2, h2, w3, b3, out_w_bytes, out_w_scale, out_b, out):
+    nc = tc.nc
+    with ExitStack() as ctx:
+        keep = ctx.enter_context(tc.tile_pool(name="keep", bufs=1))
+        work = ctx.enter_context(tc.tile_pool(name="work", bufs=3))
+        ps = ctx.enter_context(tc.psum_pool(name="ps", bufs=1))
+        ctx.enter_context(tc.manual_schedule())
+
+        x_sb = keep.tile([P, NT, F * D], BF16, name="x_sb")
+        nc.sync.dma_start(out=x_sb[:], in_=x.rearrange("(t n) f d -> n t (f d)", n=P))
+        h2_sb = []
+        x12_sb = []
+        for t in range(NT):
+            h2_sb.append(keep.tile([P, G, D], BF16, name="h2_%d" % t))
+            x12_sb.append(keep.tile([P, 2 * G, D], BF16, name="x12_%d" % t))
+
+        def load_h2(t):
+            rows = h2[t * P:(t + 1) * P].rearrange("n (b u w) d -> u n b (w d)", u=2, w=16)
+            for u in range(2):
+                nc.sync.dma_start(
+                    out=h2_sb[t][:, u * 64:(u + 1) * 64, :].rearrange("n (b w) d -> n b (w d)", w=16),
+                    in_=rows[u])
+
+        def load_x12(t):
+            nc.sync.dma_start(out=x12_sb[t][:, 0:G, :], in_=x1[t * P:(t + 1) * P])
+            nc.sync.dma_start(out=x12_sb[t][:, G:2 * G, :], in_=x2[t * P:(t + 1) * P])
+
+        load_h2(0)
+        w_raw = keep.tile([P, 2, F * G], BF16, name="w_raw")
+        nc.sync.dma_start(out=w_raw[:], in_=w3.rearrange("(c o) f g -> o c (f g)", o=P))
+        load_h2(1)
+        load_x12(0)
+        ow_raw = keep.tile([P, 4 * NOUT], U8, name="ow_raw")
+        nc.sync.dma_start(out=ow_raw[:], in_=out_w_bytes.rearrange("(p j) n -> p (j n)", j=4))
+        ow_scale = keep.tile([P, 4], F32, name="ow_scale")
+        nc.sync.dma_start(out=ow_scale[:], in_=out_w_scale.rearrange("(p j) o -> p (j o)", j=4))
+        load_h2(2)
+        load_x12(1)
+        load_h2(3)
+        load_x12(2)
+        load_x12(3)
+        b3_row = keep.tile([P, OC], BF16, name="b3_row")
+        nc.gpsimd.dma_start(out=b3_row[:], in_=b3.partition_broadcast(P))
+        ob_row = keep.tile([P, NOUT], BF16, name="ob_row")
+        nc.gpsimd.dma_start(out=ob_row[:], in_=out_b.partition_broadcast(P))
+
+        ident_f = keep.tile([P, P], F32, name="ident_f")
+        make_identity(nc, ident_f[:])
+        ident_b = keep.tile([P, P], BF16, name="ident_b")
+        make_identity(nc, ident_b[:])
+        warm = keep.tile([P, 1], F32, name="warm")
+        nc.vector.memset(warm[:], 0.0)
+        nc.scalar.activation(out=warm[:], in_=warm[:], func=ACT.Relu)
+
+        x_pair = keep.tile([P, NT, F, D, 2], BF16, name="x_pair")
+        nc.vector.tensor_copy(
+            out=x_pair[:].rearrange("n t f d e -> n (t f d) e"),
+            in_=x_sb[:].rearrange("n t k -> n (t k)").unsqueeze(2).to_broadcast([P, NT * F * D, 2]))
+
+        h2r = {}
+        p_sb = {}
+        q_in = {}
+        codes = {}
+        scales = {}
+        tr = {}
+        z = {}
+        y = {}
+        pb = {}
+
+        def arrange(g, b, eng):
+            t, d0 = g // 4, (g % 4) * GD + b * 4
+            if b == 0:
+                h2r[g] = work.tile([P, GD, G], BF16, name="h2r", bufs=3)
+            dst = h2r[g][:, b * 4:b * 4 + 4, :].rearrange("n i g -> n g i")
+            src = h2_sb[t][:, :, d0:d0 + 4]
+            if eng == 0:
+                nc.vector.tensor_copy(out=dst, in_=src)
+            else:
+                nc.scalar.copy(out=dst, in_=src)
+
+        def product(g, fs, d0, nd):
+            t, dg = g // 4, (g % 4) * GD
+            if g not in p_sb:
+                p_sb[g] = work.tile([P, GD, 2, F, 64], BF16, name="p_sb", bufs=3)
+            for f in fs:
+                nc.vector.tensor_tensor(
+                    out=p_sb[g][:, d0:d0 + nd, :, f, :],
+                    in0=h2r[g][:, d0:d0 + nd, :].rearrange("n d (u k) -> n d u k", u=2),
+                    in1=x_pair[:, t, f, dg + d0:dg + d0 + nd, :].unsqueeze(2).to_broadcast([P, nd, 64, 2]),
+                    op=ALU.mult)
+
+        def transposes(c):
+            words = p_sb[c // 2][:].rearrange("n d u f w -> n (d u f w)").bitcast(F32)
+            for h in range(2):
+                tr[c, h] = ps.tile([P, 2, 2, P], F32, name="tr", bufs=3)
+                for i in range(2):
+                    for u in range(2):
+                        w0 = (((c % 2) * CD + h * 2 + i) * 2 + u) * P
+                        nc.tensor.transpose(tr[c, h][:, i, u, :], words[:, w0:w0 + P], ident_f[:])
+
+        def empty(c, h):
+            if h == 0:
+                q_in[c] = work.tile([P, CD * P * 4], BF16, name="q_in", bufs=3, align_bytes=64)
+            words = q_in[c][:].bitcast(F32)
+            nc.scalar.copy(
+                out=words[:, h * 512:(h + 1) * 512].rearrange("p (d n u) -> p d n u", d=2, u=2),
+                in_=tr[c, h][:].rearrange("p d u n -> p d n u"))
+
+        def quantize(c):
+            codes[c] = work.tile([P, CD * P], U32, name="codes", bufs=4, align_bytes=64)
+            scales[c] = work.tile([P, CD * P], U8, name="scales", bufs=4, align_bytes=64)
+            nc.vector.quantize_mx(out=codes[c][:].bitcast(FP8X4), scales=scales[c][:], in_=q_in[c][:])
+
+        def layer(c):
+            for o in range(2):
+                z[c, o] = ps.tile([P, CD * P], F32, name="z", bufs=3)
+                nc.tensor.matmul_mx(
+                    out=z[c, o][:],
+                    lhsT=w_codes[:, o * P:(o + 1) * P].bitcast(FP8X4), lhsT_scale=w_scales[:, o * P:(o + 1) * P],
+                    rhs=codes[c][:].bitcast(FP8X4), rhs_scale=scales[c][:], start=True, stop=True)
+
+        def relu(c, o):
+            if o == 0:
+                y[c] = work.tile([P, 2, CD * P], F32, name="y", bufs=4)
+            nc.scalar.activation(out=y[c][:, o, :], in_=z[c, o][:], func=ACT.Relu, bias=b3_col[:, o:o + 1])
+
+        def pool(c):
+            t = c // PER_NT
+            if c % PER_NT == 0:
+                pb[t] = ps.tile([P, FINAL], F32, name="pb", bufs=1)
+            for o in range(2):
+                for i in range(CD):
+                    nc.tensor.matmul(
+                        pb[t][:, 2 * G + o * P:2 * G + (o + 1) * P],
+                        lhsT=y[c][:, o, i * P:(i + 1) * P], rhs=ident_f[:], is_transpose=True,
+                        start=(c % PER_NT == 0 and o == 0 and i == 0),
+                        stop=(c % PER_NT == PER_NT - 1 and o == 1 and i == CD - 1))
+
+        xa = {}
+        xa_sb = {}
+        xr = {}
+        xr_sb = {}
+        xp = {}
+
+        def x_plain(t, i0):
+            if i0 == 0:
+                xa[t] = ps.tile([P, 2 * G, 2], F32, name="xm", bufs=1)
+            for i in range(i0, i0 + 2):
+                nc.tensor.matmul(xa[t][:], lhsT=ident_b[:], rhs=x12_sb[t][:, :, 2 * i:2 * i + 2],
+                                 start=(i == 0), stop=(i == PLAIN_D // 2 - 1))
+
+        def x_plain_out(t):
+            xa_sb[t] = work.tile([P, 2 * G], F32, name="xa_sb", bufs=2)
+            nc.vector.tensor_reduce(out=xa_sb[t][:], in_=xa[t][:], axis=AX.X, op=ALU.add)
+
+        def x_pairs(t, k):
+            if k == 0:
+                xp[t] = work.tile([P, PAIRS, 2 * G], F32, name="xp", bufs=2)
+            i0, n, c0, c1 = ((0, 4, 0, G), (0, 4, G, 2 * G), (4, 4, 0, G), (4, 4, G, 2 * G), (8, 2, 0, 2 * G))[k]
+            a = PLAIN_D + i0
+            nc.vector.tensor_tensor(
+                out=xp[t][:, i0:i0 + n, c0:c1].rearrange("n i c -> n c i"),
+                in0=x12_sb[t][:, c0:c1, a:a + n],
+                in1=x12_sb[t][:, c0:c1, a + PAIRS:a + PAIRS + n], op=ALU.add)
+
+        def x_rest(t, o):
+            if o == 0:
+                xr[t] = ps.tile([P, 2, P], F32, name="xm", bufs=1)
+            for i in range(PAIRS):
+                nc.tensor.matmul(
+                    xr[t][:, o, :], lhsT=xp[t][:, i, o * P:(o + 1) * P], rhs=ident_f[:], is_transpose=True,
+                    start=(o == 0 and i == 0), stop=(o == 1 and i == PAIRS - 1))
+
+        def x_rest_out(t):
+            xr_sb[t] = work.tile([P, 2, P], F32, name="xr_sb", bufs=2)
+            nc.scalar.copy(out=xr_sb[t][:], in_=xr[t][:])
+
+        def x_rest_back(t):
+            for o in range(2):
+                nc.tensor.matmul(pb[t][:, o * P:(o + 1) * P], lhsT=xr_sb[t][:, o, :], rhs=ident_f[:],
+                                 is_transpose=True, start=False, stop=False)
+
+        pooled = {}
+        ftr = {}
+        fq = {}
+        fcodes = {}
+        fscales = {}
+
+        def fin_pool(t):
+            pooled[t] = work.tile([P, FINAL], BF16, name="pooled", bufs=2)
+            nc.vector.tensor_tensor(out=pooled[t][:, 0:2 * G], in0=pb[t][:, 0:2 * G], in1=xa_sb[t][:], op=ALU.add)
+            nc.scalar.copy(out=pooled[t][:, 2 * G:FINAL], in_=pb[t][:, 2 * G:FINAL])
+
+        def fin_transpose(t):
+            words = pooled[t][:].bitcast(F32)
+            ftr[t] = ps.tile([P, 2, P], F32, name="tr", bufs=3)
+            for u in range(2):
+                nc.tensor.transpose(ftr[t][:, u, :], words[:, u:FINAL // 2:2], ident_f[:])
+
+        def fin_empty(t):
+            fq[t] = work.tile([P, 4 * P], BF16, name="fq", bufs=2, align_bytes=64)
+            nc.scalar.copy(out=fq[t][:].bitcast(F32).rearrange("p (n u) -> p n u", u=2),
+                           in_=ftr[t][:].rearrange("p u n -> p n u"))
+
+        def fin_quantize(t):
+            fcodes[t] = work.tile([P, P], U32, name="fcodes", bufs=2, align_bytes=64)
+            fscales[t] = work.tile([P, P], U8, name="fscales", bufs=2, align_bytes=64)
+            nc.vector.quantize_mx(out=fcodes[t][:].bitcast(FP8X4), scales=fscales[t][:], in_=fq[t][:])
+
+        def fin_out(t):
+            acc = ps.tile([P, NOUT], F32, name="z", bufs=3)
+            nc.tensor.matmul_mx(out=acc[:], lhsT=fcodes[t][:].bitcast(FP8X4), lhsT_scale=fscales[t][:],
+                                rhs=ow_codes[:].bitcast(FP8X4), rhs_scale=ow_scales[:], start=True, stop=True)
+            res = work.tile([P, NOUT], F32, name="res", bufs=2)
+            nc.vector.tensor_tensor(out=res[:], in0=acc[:], in1=ob_row[:], op=ALU.add)
+            nc.sync.dma_start(out=out[t * P:(t + 1) * P, :], in_=res[:])
+
+        arrange(0, 0, 0)
+        arrange(0, 1, 1)
+        product(0, range(F), 0, CD)
+
+        w_perm = keep.tile([P, 2, 2, 16, 16], BF16, name="w_perm")
+        for u in range(2):
+            nc.scalar.copy(out=w_perm[:, :, u, :, :],
+                           in_=w_raw[:].rearrange("o c (b u w) -> o u c b w", u=2, w=16)[:, u])
+        transposes(0)
+        empty(0, 0)
+        empty(0, 1)
+        product(0, range(F), CD, CD)
+        arrange(1, 0, 0)
+        arrange(1, 1, 1)
+
+        b3_ps = ps.tile([P, 2, P], BF16, name="xm", bufs=1)
+        for o in range(2):
+            nc.tensor.transpose(b3_ps[:, o, :], b3_row[:, o * P:(o + 1) * P], ident_b[:])
+        b3_col = keep.tile([P, 2], F32, name="b3_col")
+        nc.scalar.copy(out=b3_col[:], in_=b3_ps[:, :, 0])
+
+        w_tr = ps.tile([P, 2, 2, P], F32, name="tr", bufs=3)
+        w_words = w_perm[:].rearrange("o c u b w -> o (c u b w)").bitcast(F32)
+        for o in range(2):
+            for u in range(2):
+                nc.tensor.transpose(w_tr[:, o, u, :], w_words[:, (2 * o + u) * P:(2 * o + u + 1) * P], ident_f[:])
+        w_q = keep.tile([P, 2 * P * 4], BF16, name="w_q", align_bytes=64)
+        nc.scalar.copy(out=w_q[:].bitcast(F32).rearrange("p (c o u) -> p c o u", c=2, u=2),
+                       in_=w_tr[:].rearrange("p c u o -> p c o u"))
+        w_codes = keep.tile([P, OC], U32, name="w_codes", align_bytes=64)
+        w_scales = keep.tile([P, OC], U8, name="w_scales", align_bytes=64)
+        quantize(0)
+        nc.vector.quantize_mx(out=w_codes[:].bitcast(FP8X4), scales=w_scales[:], in_=w_q[:])
+        product(1, range(F), 0, GD)
+        arrange(2, 0, 0)
+        arrange(2, 1, 1)
+
+        ow_q = keep.tile([P, NOUT, 4], BF16, name="ow_q", align_bytes=64)
+        ow_codes = keep.tile([P, NOUT], U32, name="ow_codes", align_bytes=64)
+        ow_scales = keep.tile([P, NOUT], U8, name="ow_scales", align_bytes=64)
+
+        for s in range(1, CHUNKS + 6):
+            for t in range(NT):
+                if s - PER_NT * t == 12:
+                    fin_pool(t)
+            if 0 <= s - 3 < CHUNKS:
+                relu(s - 3, 0)
+            if s < CHUNKS:
+                transposes(s)
+                empty(s, 0)
+            if 0 <= s - 3 < CHUNKS:
+                relu(s - 3, 1)
+            if s < CHUNKS:
+                empty(s, 1)
+            for t in range(NT):
+                o = s - PER_NT * t
+                if o in (7, 8):
+                    x_rest(t, o - 7)
+                if o == 9:
+                    x_rest_out(t)
+                if o == 10:
+                    x_rest_back(t)
+            if 0 <= s - 4 < CHUNKS:
+                pool(s - 4)
+            for t in range(NT):
+                o = s - PER_NT * t
+                if o in (2, 3, 4):
+                    x_plain(t, 2 * (o - 2))
+            if 0 <= s - 2 < CHUNKS:
+                layer(s - 2)
+            if 1 < s <= CHUNKS:
+                quantize(s - 1)
+            g = (s + 3) // 2
+            if s % 2 == 1:
+                if g < GROUPS:
+                    product(g, (0, 1), 0, GD)
+            else:
+                g = (s + 2) // 2
+                if g < GROUPS:
+                    product(g, (2, 3), 0, GD)
+            ga, b = (s + 5) // 2, (s + 5) % 2
+            if ga < GROUPS:
+                arrange(ga, b, 0)
+            for t in range(NT):
+                o = s - PER_NT * t
+                if 2 <= o <= 6:
+                    x_pairs(t, o - 2)
+                if o == 5:
+                    x_plain_out(t)
+                if o == 12:
+                    fin_transpose(t)
+                    fin_empty(t)
+                if o == 13:
+                    fin_quantize(t)
+                    fin_out(t)
+            if s == 9:
+                for j in range(4):
+                    nc.vector.tensor_scalar(
+                        out=ow_q[:, :, j], in0=ow_raw[:, j * NOUT:(j + 1) * NOUT].bitcast(FP8),
+                        scalar1=ow_scale[:, j:j + 1], scalar2=None, op0=ALU.mult)
+                nc.vector.quantize_mx(out=ow_codes[:].bitcast(FP8X4), scales=ow_scales[:],
+                                      in_=ow_q[:].rearrange("p n j -> p (n j)"))

@@ -22,9 +22,28 @@ NT = B // P
 CD = 4
 CHUNKS = NT * D // CD
 PER_NT = D // CD
-GD = 8
-GROUPS = CHUNKS // 2
+SIZES = [1, 1, 2] + [2] * 2 + [4] * 6
+GROUPS = [(sum(SIZES[:g]), n) for g, n in enumerate(SIZES)]
+PRODUCTS = [(c - n + f * n // F, g, f) for g, (c, n) in enumerate(GROUPS) for f in range(F)]
+GROUP_OF = {c + i: (g, i) for g, (c, n) in enumerate(GROUPS) for i in range(n)}
 PLAIN_D = 12
+PAIRED = ((15, 0), (17, 1), (18, 0), (23, 0), (24, 0), (25, 0), (25, 1), (26, 0), (26, 1), (27, 0), (29, 0), (29, 1), (30, 0), (30, 1), (31, 0), (31, 1))
+Z_IN_TR = 30
+EV_ON_V = ((16, 1), (31, 1))
+ARR_S = (3, 4, 5, 7, 8, 12, 15, 18, 22, 24, 28, 31)
+HALF_ON_V = 0
+A_AHEAD = 8
+S_OW = 12
+PIECES = ((0, 4, 0, G), (0, 4, G, 2 * G), (4, 4, 0, G), (4, 4, G, 2 * G), (8, 2, 0, 2 * G))
+O_PAIR = ((3, 5, 6, 7, 8), (1, 3, 4, 4, 6), (1, 2, 4, 6, 6), (-1, 1, 3, 4, 5))
+O_REST = ((4, 6, 7, 8, 9), (3, 4, 5, 7, 7), (3, 4, 5, 8, 8), (2, 3, 4, 6, 7))
+O_REST_OUT = (10, 9, 9, 9)
+O_REST_BACK = (11, 11, 11, 10)
+O_PLAIN = ((5, 5, 7, 8, 10, 10), (5, 6, 7, 8, 9, 10), (5, 6, 7, 7, 9, 9), (5, 6, 7, 8, 10, 10))
+O_PLAIN_OUT = (8, 8, 8, 7)
+O_FIN = (12, 13, 13, 14, 14)
+O_LAST = (12, 12, 12, 13, 13)
+LQ, LM, LR, LW = 1, 2, 3, 4
 PAIRS = (D - PLAIN_D) // 2
 
 
@@ -37,12 +56,11 @@ def tile_cin_pb_t_kernel(tc, x, x1, x2, h2, w3, b3, out_w_bytes, out_w_scale, ou
         ctx.enter_context(tc.manual_schedule())
 
         x_sb = keep.tile([P, NT, F * D], BF16, name="x_sb")
-        nc.sync.dma_start(out=x_sb[:], in_=x.rearrange("(t n) f d -> n t (f d)", n=P))
         h2_sb = []
-        x12_sb = []
+        x12_sb = {}
         for t in range(NT):
-            h2_sb.append(keep.tile([P, G, D], BF16, name="h2_%d" % t))
-            x12_sb.append(keep.tile([P, 2 * G, D], BF16, name="x12_%d" % t))
+            h2_sb.append(work.tile([P, G, D], BF16, name="h2_sb", bufs=4))
+
 
         def load_h2(t):
             rows = h2[t * P:(t + 1) * P].rearrange("n (b u w) d -> u n b (w d)", u=2, w=16)
@@ -50,16 +68,19 @@ def tile_cin_pb_t_kernel(tc, x, x1, x2, h2, w3, b3, out_w_bytes, out_w_scale, ou
                 nc.sync.dma_start(
                     out=h2_sb[t][:, u * 64:(u + 1) * 64, :].rearrange("n (b w) d -> n b (w d)", w=16),
                     in_=rows[u])
+                if t == 0 and u == 0:
+                    nc.sync.dma_start(out=x_sb[:], in_=x.rearrange("(t n) f d -> n t (f d)", n=P))
 
         def load_x12(t):
+            x12_sb[t] = work.tile([P, 2 * G, D], BF16, name="x12_sb", bufs=3)
             nc.sync.dma_start(out=x12_sb[t][:, 0:G, :], in_=x1[t * P:(t + 1) * P])
             nc.sync.dma_start(out=x12_sb[t][:, G:2 * G, :], in_=x2[t * P:(t + 1) * P])
 
         load_h2(0)
         w_raw = keep.tile([P, 2, F * G], BF16, name="w_raw")
         nc.sync.dma_start(out=w_raw[:], in_=w3.rearrange("(c o) f g -> o c (f g)", o=P))
-        load_h2(1)
         load_x12(0)
+        load_h2(1)
         ow_raw = keep.tile([P, 4 * NOUT], U8, name="ow_raw")
         nc.sync.dma_start(out=ow_raw[:], in_=out_w_bytes.rearrange("(p j) n -> p (j n)", j=4))
         ow_scale = keep.tile([P, 4], F32, name="ow_scale")
@@ -68,7 +89,6 @@ def tile_cin_pb_t_kernel(tc, x, x1, x2, h2, w3, b3, out_w_bytes, out_w_scale, ou
         load_x12(1)
         load_h2(3)
         load_x12(2)
-        load_x12(3)
         b3_row = keep.tile([P, OC], BF16, name="b3_row")
         nc.gpsimd.dma_start(out=b3_row[:], in_=b3.partition_broadcast(P))
         ob_row = keep.tile([P, NOUT], BF16, name="ob_row")
@@ -83,9 +103,11 @@ def tile_cin_pb_t_kernel(tc, x, x1, x2, h2, w3, b3, out_w_bytes, out_w_scale, ou
         nc.scalar.activation(out=warm[:], in_=warm[:], func=ACT.Relu)
 
         x_pair = keep.tile([P, NT, F, D, 2], BF16, name="x_pair")
-        nc.vector.tensor_copy(
-            out=x_pair[:].rearrange("n t f d e -> n (t f d) e"),
-            in_=x_sb[:].rearrange("n t k -> n (t k)").unsqueeze(2).to_broadcast([P, NT * F * D, 2]))
+
+        def pair_x():
+            nc.vector.tensor_copy(
+                out=x_pair[:].rearrange("n t f d e -> n (t f d) e"),
+                in_=x_sb[:].rearrange("n t k -> n (t k)").unsqueeze(2).to_broadcast([P, NT * F * D, 2]))
 
         h2r = {}
         p_sb = {}
@@ -97,22 +119,25 @@ def tile_cin_pb_t_kernel(tc, x, x1, x2, h2, w3, b3, out_w_bytes, out_w_scale, ou
         y = {}
         pb = {}
 
-        def arrange(g, b, eng):
-            t, d0 = g // 4, (g % 4) * GD + b * 4
-            if b == 0:
-                h2r[g] = work.tile([P, GD, G], BF16, name="h2r", bufs=3)
-            dst = h2r[g][:, b * 4:b * 4 + 4, :].rearrange("n i g -> n g i")
-            src = h2_sb[t][:, :, d0:d0 + 4]
+        def arrange(c, eng, g0=0, g1=G):
+            t, d0 = c // PER_NT, c % PER_NT * CD
+            g, b = GROUP_OF[c]
+            if g not in h2r:
+                h2r[g] = work.tile([P, 4 * CD, G], BF16, name="h2r", bufs=5)
+            dst = h2r[g][:, b * CD:b * CD + CD, g0:g1].rearrange("n i g -> n g i")
+            src = h2_sb[t][:, g0:g1, d0:d0 + 4]
             if eng == 0:
                 nc.vector.tensor_copy(out=dst, in_=src)
             else:
                 nc.scalar.copy(out=dst, in_=src)
 
-        def product(g, fs, d0, nd):
-            t, dg = g // 4, (g % 4) * GD
+        def product(g, f):
+            c, n = GROUPS[g]
+            t, dg = c // PER_NT, c % PER_NT * CD
+            d0, nd = 0, n * CD
             if g not in p_sb:
-                p_sb[g] = work.tile([P, GD, 2, F, 64], BF16, name="p_sb", bufs=3)
-            for f in fs:
+                p_sb[g] = work.tile([P, 4 * CD, 2, F, 64], BF16, name="p_sb", bufs=3)
+            if True:
                 nc.vector.tensor_tensor(
                     out=p_sb[g][:, d0:d0 + nd, :, f, :],
                     in0=h2r[g][:, d0:d0 + nd, :].rearrange("n d (u k) -> n d u k", u=2),
@@ -120,21 +145,25 @@ def tile_cin_pb_t_kernel(tc, x, x1, x2, h2, w3, b3, out_w_bytes, out_w_scale, ou
                     op=ALU.mult)
 
         def transposes(c):
-            words = p_sb[c // 2][:].rearrange("n d u f w -> n (d u f w)").bitcast(F32)
+            g, b = GROUP_OF[c]
+            words = p_sb[g][:].rearrange("n d u f w -> n (d u f w)").bitcast(F32)
             for h in range(2):
                 tr[c, h] = ps.tile([P, 2, 2, P], F32, name="tr", bufs=3)
                 for i in range(2):
                     for u in range(2):
-                        w0 = (((c % 2) * CD + h * 2 + i) * 2 + u) * P
+                        w0 = ((b * CD + h * 2 + i) * 2 + u) * P
                         nc.tensor.transpose(tr[c, h][:, i, u, :], words[:, w0:w0 + P], ident_f[:])
 
         def empty(c, h):
             if h == 0:
                 q_in[c] = work.tile([P, CD * P * 4], BF16, name="q_in", bufs=3, align_bytes=64)
             words = q_in[c][:].bitcast(F32)
-            nc.scalar.copy(
-                out=words[:, h * 512:(h + 1) * 512].rearrange("p (d n u) -> p d n u", d=2, u=2),
-                in_=tr[c, h][:].rearrange("p d u n -> p d n u"))
+            dst = words[:, h * 512:(h + 1) * 512].rearrange("p (d n u) -> p d n u", d=2, u=2)
+            src = tr[c, h][:].rearrange("p d u n -> p d n u")
+            if (c, h) in EV_ON_V:
+                nc.vector.tensor_copy(out=dst, in_=src)
+            else:
+                nc.scalar.copy(out=dst, in_=src)
 
         def quantize(c):
             codes[c] = work.tile([P, CD * P], U32, name="codes", bufs=4, align_bytes=64)
@@ -143,7 +172,10 @@ def tile_cin_pb_t_kernel(tc, x, x1, x2, h2, w3, b3, out_w_bytes, out_w_scale, ou
 
         def layer(c):
             for o in range(2):
-                z[c, o] = ps.tile([P, CD * P], F32, name="z", bufs=3)
+                if c >= Z_IN_TR:
+                    z[c, o] = ps.tile([P, CD * P], F32, name="tr", bufs=3)
+                else:
+                    z[c, o] = ps.tile([P, CD * P], F32, name="z", bufs=3)
                 nc.tensor.matmul_mx(
                     out=z[c, o][:],
                     lhsT=w_codes[:, o * P:(o + 1) * P].bitcast(FP8X4), lhsT_scale=w_scales[:, o * P:(o + 1) * P],
@@ -152,54 +184,56 @@ def tile_cin_pb_t_kernel(tc, x, x1, x2, h2, w3, b3, out_w_bytes, out_w_scale, ou
         def relu(c, o):
             if o == 0:
                 y[c] = work.tile([P, 2, CD * P], F32, name="y", bufs=4)
-            nc.scalar.activation(out=y[c][:, o, :], in_=z[c, o][:], func=ACT.Relu, bias=b3_col[:, o:o + 1])
+            w = CD * P // 2 if (c, o) in PAIRED else CD * P
+            nc.scalar.activation(out=y[c][:, o, 0:w], in_=z[c, o][:, 0:w], func=ACT.Relu, bias=b3_col[:, o:o + 1])
+
+        def relu_pair(c, o):
+            if (c, o) in PAIRED:
+                h = CD * P // 2
+                nc.vector.scalar_tensor_tensor(
+                    out=y[c][:, o, h:2 * h], in0=z[c, o][:, h:2 * h], scalar=nb3_col[:, o:o + 1],
+                    in1=y[c][:, o, 0:h], op0=ALU.max, op1=ALU.add)
 
         def pool(c):
             t = c // PER_NT
             if c % PER_NT == 0:
                 pb[t] = ps.tile([P, FINAL], F32, name="pb", bufs=1)
             for o in range(2):
-                for i in range(CD):
+                i0 = CD // 2 if (c, o) in PAIRED else 0
+                for i in range(i0, CD):
                     nc.tensor.matmul(
                         pb[t][:, 2 * G + o * P:2 * G + (o + 1) * P],
                         lhsT=y[c][:, o, i * P:(i + 1) * P], rhs=ident_f[:], is_transpose=True,
-                        start=(c % PER_NT == 0 and o == 0 and i == 0),
+                        start=(c % PER_NT == 0 and o == 0 and i == i0),
                         stop=(c % PER_NT == PER_NT - 1 and o == 1 and i == CD - 1))
 
-        xa = {}
-        xa_sb = {}
         xr = {}
         xr_sb = {}
         xp = {}
 
-        def x_plain(t, i0):
-            if i0 == 0:
-                xa[t] = ps.tile([P, 2 * G, 2], F32, name="xm", bufs=1)
-            for i in range(i0, i0 + 2):
-                nc.tensor.matmul(xa[t][:], lhsT=ident_b[:], rhs=x12_sb[t][:, :, 2 * i:2 * i + 2],
-                                 start=(i == 0), stop=(i == PLAIN_D // 2 - 1))
-
-        def x_plain_out(t):
-            xa_sb[t] = work.tile([P, 2 * G], F32, name="xa_sb", bufs=2)
-            nc.vector.tensor_reduce(out=xa_sb[t][:], in_=xa[t][:], axis=AX.X, op=ALU.add)
+        def x_plain(t, i):
+            for d in (2 * i, 2 * i + 1):
+                nc.tensor.matmul(pb[t][:, 0:2 * G], lhsT=ident_b[:], rhs=x12_sb[t][:, :, d], start=False, stop=False)
 
         def x_pairs(t, k):
             if k == 0:
                 xp[t] = work.tile([P, PAIRS, 2 * G], F32, name="xp", bufs=2)
-            i0, n, c0, c1 = ((0, 4, 0, G), (0, 4, G, 2 * G), (4, 4, 0, G), (4, 4, G, 2 * G), (8, 2, 0, 2 * G))[k]
+            i0, n, c0, c1 = PIECES[k]
             a = PLAIN_D + i0
             nc.vector.tensor_tensor(
                 out=xp[t][:, i0:i0 + n, c0:c1].rearrange("n i c -> n c i"),
                 in0=x12_sb[t][:, c0:c1, a:a + n],
                 in1=x12_sb[t][:, c0:c1, a + PAIRS:a + PAIRS + n], op=ALU.add)
 
-        def x_rest(t, o):
-            if o == 0:
-                xr[t] = ps.tile([P, 2, P], F32, name="xm", bufs=1)
-            for i in range(PAIRS):
-                nc.tensor.matmul(
-                    xr[t][:, o, :], lhsT=xp[t][:, i, o * P:(o + 1) * P], rhs=ident_f[:], is_transpose=True,
-                    start=(o == 0 and i == 0), stop=(o == 1 and i == PAIRS - 1))
+        def x_rest(t, k):
+            i0, n, c0, c1 = PIECES[k]
+            if (i0, c0) == (0, 0):
+                xr[t] = ps.tile([P, 2, P], F32, name="xr", bufs=1)
+            for o in range(c0 // G, c1 // G):
+                for i in range(i0, i0 + n):
+                    nc.tensor.matmul(
+                        xr[t][:, o, :], lhsT=xp[t][:, i, o * P:(o + 1) * P], rhs=ident_f[:], is_transpose=True,
+                        start=(o == 0 and i == 0), stop=(o == 1 and i == PAIRS - 1))
 
         def x_rest_out(t):
             xr_sb[t] = work.tile([P, 2, P], F32, name="xr_sb", bufs=2)
@@ -218,8 +252,16 @@ def tile_cin_pb_t_kernel(tc, x, x1, x2, h2, w3, b3, out_w_bytes, out_w_scale, ou
 
         def fin_pool(t):
             pooled[t] = work.tile([P, FINAL], BF16, name="pooled", bufs=2)
-            nc.vector.tensor_tensor(out=pooled[t][:, 0:2 * G], in0=pb[t][:, 0:2 * G], in1=xa_sb[t][:], op=ALU.add)
-            nc.scalar.copy(out=pooled[t][:, 2 * G:FINAL], in_=pb[t][:, 2 * G:FINAL])
+            nc.vector.tensor_copy(out=pooled[t][:, 0:2 * G], in_=pb[t][:, 0:2 * G])
+            for o in range(2):
+                left = sum([CD // 2 for c, oo in PAIRED if c // PER_NT == t and oo == o])
+                cols = slice(2 * G + o * P, 2 * G + (o + 1) * P)
+                if left:
+                    nc.vector.scalar_tensor_tensor(
+                        out=pooled[t][:, cols], in0=b3_row[:, o * P:(o + 1) * P], scalar=float(left),
+                        in1=pb[t][:, cols], op0=ALU.mult, op1=ALU.add)
+                else:
+                    nc.scalar.copy(out=pooled[t][:, cols], in_=pb[t][:, cols])
 
         def fin_transpose(t):
             words = pooled[t][:].bitcast(F32)
@@ -237,35 +279,40 @@ def tile_cin_pb_t_kernel(tc, x, x1, x2, h2, w3, b3, out_w_bytes, out_w_scale, ou
             fscales[t] = work.tile([P, P], U8, name="fscales", bufs=2, align_bytes=64)
             nc.vector.quantize_mx(out=fcodes[t][:].bitcast(FP8X4), scales=fscales[t][:], in_=fq[t][:])
 
-        def fin_out(t):
-            acc = ps.tile([P, NOUT], F32, name="z", bufs=3)
-            nc.tensor.matmul_mx(out=acc[:], lhsT=fcodes[t][:].bitcast(FP8X4), lhsT_scale=fscales[t][:],
+        facc = {}
+
+        def fin_mm(t):
+            facc[t] = ps.tile([P, NOUT], F32, name="z", bufs=3)
+            nc.tensor.matmul_mx(out=facc[t][:], lhsT=fcodes[t][:].bitcast(FP8X4), lhsT_scale=fscales[t][:],
                                 rhs=ow_codes[:].bitcast(FP8X4), rhs_scale=ow_scales[:], start=True, stop=True)
+
+        def fin_out(t):
             res = work.tile([P, NOUT], F32, name="res", bufs=2)
-            nc.vector.tensor_tensor(out=res[:], in0=acc[:], in1=ob_row[:], op=ALU.add)
+            nc.vector.tensor_tensor(out=res[:], in0=facc[t][:], in1=ob_row[:], op=ALU.add)
             nc.sync.dma_start(out=out[t * P:(t + 1) * P, :], in_=res[:])
 
-        arrange(0, 0, 0)
-        arrange(0, 1, 1)
-        product(0, range(F), 0, CD)
-
+        arrange(0, 0, 0, G // 2)
+        pair_x()
+        for c in range(1, HALF_ON_V + 1):
+            arrange(c, 0, 0, G // 2)
+        arrange(0, 0, G // 2, G)
+        arrange(1, 1, G // 2 if HALF_ON_V >= 1 else 0)
+        for f in range(F):
+            product(0, f)
         w_perm = keep.tile([P, 2, 2, 16, 16], BF16, name="w_perm")
-        for u in range(2):
-            nc.scalar.copy(out=w_perm[:, :, u, :, :],
-                           in_=w_raw[:].rearrange("o c (b u w) -> o u c b w", u=2, w=16)[:, u])
         transposes(0)
+        arrange(2, 1, G // 2 if HALF_ON_V >= 2 else 0)
+        arrange(3, 1, G // 2 if HALF_ON_V >= 3 else 0)
         empty(0, 0)
         empty(0, 1)
-        product(0, range(F), CD, CD)
-        arrange(1, 0, 0)
-        arrange(1, 1, 1)
-
-        b3_ps = ps.tile([P, 2, P], BF16, name="xm", bufs=1)
+        for f in range(F):
+            product(1, f)
+        for u in range(2):
+            nc.vector.tensor_copy(out=w_perm[:, :, u, :, :],
+                                  in_=w_raw[:].rearrange("o c (b u w) -> o u c b w", u=2, w=16)[:, u])
+        b3_ps = ps.tile([P, 2, P], BF16, name="xr", bufs=1)
         for o in range(2):
             nc.tensor.transpose(b3_ps[:, o, :], b3_row[:, o * P:(o + 1) * P], ident_b[:])
-        b3_col = keep.tile([P, 2], F32, name="b3_col")
-        nc.scalar.copy(out=b3_col[:], in_=b3_ps[:, :, 0])
-
         w_tr = ps.tile([P, 2, 2, P], F32, name="tr", bufs=3)
         w_words = w_perm[:].rearrange("o c u b w -> o (c u b w)").bitcast(F32)
         for o in range(2):
@@ -274,76 +321,97 @@ def tile_cin_pb_t_kernel(tc, x, x1, x2, h2, w3, b3, out_w_bytes, out_w_scale, ou
         w_q = keep.tile([P, 2 * P * 4], BF16, name="w_q", align_bytes=64)
         nc.scalar.copy(out=w_q[:].bitcast(F32).rearrange("p (c o u) -> p c o u", c=2, u=2),
                        in_=w_tr[:].rearrange("p c u o -> p c o u"))
+        b3_col = keep.tile([P, 2], F32, name="b3_col")
+        nc.scalar.copy(out=b3_col[:], in_=b3_ps[:, :, 0])
+        for f in range(F):
+            product(2, f)
+            if f == 1:
+                quantize(0)
         w_codes = keep.tile([P, OC], U32, name="w_codes", align_bytes=64)
         w_scales = keep.tile([P, OC], U8, name="w_scales", align_bytes=64)
-        quantize(0)
         nc.vector.quantize_mx(out=w_codes[:].bitcast(FP8X4), scales=w_scales[:], in_=w_q[:])
-        product(1, range(F), 0, GD)
-        arrange(2, 0, 0)
-        arrange(2, 1, 1)
+        for c in range(4, A_AHEAD + 1):
+            arrange(c, 1 if c in ARR_S else 0)
+        for st, g, f in PRODUCTS:
+            if st <= 0 and g > 2:
+                product(g, f)
 
+        nb3_col = keep.tile([P, 2], F32, name="nb3_col")
         ow_q = keep.tile([P, NOUT, 4], BF16, name="ow_q", align_bytes=64)
         ow_codes = keep.tile([P, NOUT], U32, name="ow_codes", align_bytes=64)
         ow_scales = keep.tile([P, NOUT], U8, name="ow_scales", align_bytes=64)
 
-        for s in range(1, CHUNKS + 6):
-            for t in range(NT):
-                if s - PER_NT * t == 12:
+        for s in range(1, CHUNKS + 8):
+            places = [(t, s - PER_NT * t, O_LAST if t == NT - 1 else O_FIN) for t in range(NT)]
+            for t, o, fin in places:
+                if o == fin[0]:
                     fin_pool(t)
-            if 0 <= s - 3 < CHUNKS:
-                relu(s - 3, 0)
+            if 0 <= s - LR < CHUNKS:
+                relu(s - LR, 0)
             if s < CHUNKS:
                 transposes(s)
                 empty(s, 0)
-            if 0 <= s - 3 < CHUNKS:
-                relu(s - 3, 1)
-            if s < CHUNKS:
+            if 0 <= s - LR < CHUNKS:
+                relu(s - LR, 1)
+            if s < CHUNKS and (s, 1) not in EV_ON_V:
                 empty(s, 1)
-            for t in range(NT):
-                o = s - PER_NT * t
-                if o in (7, 8):
-                    x_rest(t, o - 7)
-                if o == 9:
+            for t, o, fin in places:
+                if o == O_REST_OUT[t]:
                     x_rest_out(t)
-                if o == 10:
-                    x_rest_back(t)
-            if 0 <= s - 4 < CHUNKS:
-                pool(s - 4)
-            for t in range(NT):
-                o = s - PER_NT * t
-                if o in (2, 3, 4):
-                    x_plain(t, 2 * (o - 2))
-            if 0 <= s - 2 < CHUNKS:
-                layer(s - 2)
-            if 1 < s <= CHUNKS:
-                quantize(s - 1)
-            g = (s + 3) // 2
-            if s % 2 == 1:
-                if g < GROUPS:
-                    product(g, (0, 1), 0, GD)
-            else:
-                g = (s + 2) // 2
-                if g < GROUPS:
-                    product(g, (2, 3), 0, GD)
-            ga, b = (s + 5) // 2, (s + 5) % 2
-            if ga < GROUPS:
-                arrange(ga, b, 0)
-            for t in range(NT):
-                o = s - PER_NT * t
-                if 2 <= o <= 6:
-                    x_pairs(t, o - 2)
-                if o == 5:
-                    x_plain_out(t)
-                if o == 12:
-                    fin_transpose(t)
-                    fin_empty(t)
-                if o == 13:
-                    fin_quantize(t)
+            if s == PER_NT + 4:
+                load_x12(3)
+            for t, o, fin in places:
+                if o == fin[4] + 1 and t < NT - 1:
                     fin_out(t)
-            if s == 9:
+            for st, g, f in PRODUCTS:
+                if st == s:
+                    product(g, f)
+            if 1 <= s - LQ < CHUNKS:
+                quantize(s - LQ)
+            if (s, 1) in EV_ON_V:
+                empty(s, 1)
+            for o in range(2):
+                if 0 <= s - LR < CHUNKS:
+                    relu_pair(s - LR, o)
+            if s + A_AHEAD < CHUNKS:
+                arrange(s + A_AHEAD, 1 if s + A_AHEAD in ARR_S else 0)
+            for t, o, fin in places:
+                for k in range(5):
+                    if o == O_PAIR[t][k]:
+                        x_pairs(t, k)
+                if o == fin[3]:
+                    fin_quantize(t)
+            if s == 2:
+                nc.vector.tensor_scalar(out=nb3_col[:], in0=b3_col[:], scalar1=-1.0, scalar2=None, op0=ALU.mult)
+            if s == S_OW:
                 for j in range(4):
                     nc.vector.tensor_scalar(
                         out=ow_q[:, :, j], in0=ow_raw[:, j * NOUT:(j + 1) * NOUT].bitcast(FP8),
                         scalar1=ow_scale[:, j:j + 1], scalar2=None, op0=ALU.mult)
                 nc.vector.quantize_mx(out=ow_codes[:].bitcast(FP8X4), scales=ow_scales[:],
                                       in_=ow_q[:].rearrange("p n j -> p (n j)"))
+            for t, o, fin in places:
+                if o == fin[1]:
+                    fin_transpose(t)
+                if o == O_REST_BACK[t]:
+                    x_rest_back(t)
+            if s >= CHUNKS and 0 <= s - LM < CHUNKS:
+                layer(s - LM)
+            if 0 <= s - LW < CHUNKS:
+                pool(s - LW)
+            for t, o, fin in places:
+                for k in range(5):
+                    if o == O_REST[t][k]:
+                        x_rest(t, k)
+                for i in range(6):
+                    if o == O_PLAIN[t][i]:
+                        x_plain(t, i)
+            if s < CHUNKS and 0 <= s - LM < CHUNKS:
+                layer(s - LM)
+            for t, o, fin in places:
+                if o == fin[2]:
+                    fin_empty(t)
+                if o == fin[4]:
+                    fin_mm(t)
+                    if t == NT - 1:
+                        fin_out(t)

@@ -11,7 +11,6 @@ FP8 = mybir.dt.float8_e4m3fn
 FP8X4 = mybir.dt.float8_e4m3fn_x4
 ALU = mybir.AluOpType
 ACT = mybir.ActivationFunctionType
-AX = mybir.AxisListType
 
 B, F, D, G, OC = 512, 4, 32, 128, 256
 FINAL, NOUT = 512, 128
@@ -20,31 +19,36 @@ FLOPS = 2 * B * D * F * G * OC + 2 * B * FINAL * NOUT
 
 NT = B // P
 CD = 4
-CHUNKS = NT * D // CD
+COLS = CD * P
 PER_NT = D // CD
-SIZES = [1, 1, 2] + [2] * 2 + [4] * 6
-GROUPS = [(sum(SIZES[:g]), n) for g, n in enumerate(SIZES)]
-PRODUCTS = [(c - n + f * n // F, g, f) for g, (c, n) in enumerate(GROUPS) for f in range(F)]
-GROUP_OF = {c + i: (g, i) for g, (c, n) in enumerate(GROUPS) for i in range(n)}
+CHUNKS = NT * PER_NT
+
+SIZES = [1, 1, 2, 2, 2] + [4] * 6
+RUNS = [(sum(SIZES[:r]), size) for r, size in enumerate(SIZES)]
+RUN_OF = {c + i: (r, i) for r, (c, size) in enumerate(RUNS) for i in range(size)}
+RUN_D = 4 * CD
+PRODUCTS = [(c - size + f * size // F, r, f) for r, (c, size) in enumerate(RUNS) for f in range(F)]
+
 PLAIN_D = 12
-PAIRED = ((15, 0), (17, 1), (18, 0), (23, 0), (24, 0), (25, 0), (25, 1), (26, 0), (26, 1), (27, 0), (29, 0), (29, 1), (30, 0), (30, 1), (31, 0), (31, 1))
-Z_IN_TR = 30
-EV_ON_V = ((16, 1), (31, 1))
-ARR_S = (3, 4, 5, 7, 8, 12, 15, 18, 22, 24, 28, 31)
-HALF_ON_V = 0
-A_AHEAD = 8
-S_OW = 12
-PIECES = ((0, 4, 0, G), (0, 4, G, 2 * G), (4, 4, 0, G), (4, 4, G, 2 * G), (8, 2, 0, 2 * G))
-O_PAIR = ((3, 5, 6, 7, 8), (1, 3, 4, 4, 6), (1, 2, 4, 6, 6), (-1, 1, 3, 4, 5))
-O_REST = ((4, 6, 7, 8, 9), (3, 4, 5, 7, 7), (3, 4, 5, 8, 8), (2, 3, 4, 6, 7))
-O_REST_OUT = (10, 9, 9, 9)
-O_REST_BACK = (11, 11, 11, 10)
-O_PLAIN = ((5, 5, 7, 8, 10, 10), (5, 6, 7, 8, 9, 10), (5, 6, 7, 7, 9, 9), (5, 6, 7, 8, 10, 10))
-O_PLAIN_OUT = (8, 8, 8, 7)
-O_FIN = (12, 13, 13, 14, 14)
-O_LAST = (12, 12, 12, 13, 13)
-LQ, LM, LR, LW = 1, 2, 3, 4
 PAIRS = (D - PLAIN_D) // 2
+PIECES = ((0, 4, 0, G), (0, 4, G, 2 * G), (4, 4, 0, G), (4, 4, G, 2 * G), (8, 2, 0, 2 * G))
+
+ON_VECTOR = [(c, 1) for c in (3, 11, 19, 25, 26, 27, 29)]
+PAIRED = [(c, 0) for c in (23, 24, 25, 26, 29, 31)] + [(30, 1)]
+
+QUANTIZE, LAYER, RELU, POOL = 1, 2, 3, 4
+X_PAIRS = ((3, 4, 6, 6, 8), (1, 3, 4, 4, 6), (1, 2, 4, 6, 6), (-2, 2, 3, 4, 5))
+X_REST = ((4, 6, 7, 8, 9), (3, 5, 6, 8, 8), (3, 3, 7, 8, 8), (2, 4, 4, 5, 7))
+X_REST_OUT = (10, 10, 9, 9)
+X_REST_BACK = (11, 11, 10, 11)
+X_PLAIN = ((2, 3, 4, 5, 5, 7), (2, 3, 4, 6, 6, 6), (2, 2, 4, 5, 7, 7), (1, 2, 3, 5, 5, 6))
+X_PLAIN_OUT = (8, 9, 8, 7)
+FINISH = (12, 13, 13, 14, 14)
+FINISH_LAST = (12, 12, 12, 13, 13)
+ARRANGE_AHEAD = 8
+X12_STEP = 12
+OUT_W_STEP = 12
+Z_IN_TR = CHUNKS - 2
 
 
 def tile_cin_pb_t_kernel(tc, x, x1, x2, h2, w3, b3, out_w_bytes, out_w_scale, out_b, out):
@@ -56,38 +60,36 @@ def tile_cin_pb_t_kernel(tc, x, x1, x2, h2, w3, b3, out_w_bytes, out_w_scale, ou
         ctx.enter_context(tc.manual_schedule())
 
         x_sb = keep.tile([P, NT, F * D], BF16, name="x_sb")
-        h2_sb = []
+        h2_sb = [work.tile([P, G, D], BF16, name="h2_sb", bufs=NT) for t in range(NT)]
         x12_sb = {}
-        for t in range(NT):
-            h2_sb.append(work.tile([P, G, D], BF16, name="h2_sb", bufs=4))
 
-
-        def load_h2(t):
+        def load_h2(t, u):
             rows = h2[t * P:(t + 1) * P].rearrange("n (b u w) d -> u n b (w d)", u=2, w=16)
-            for u in range(2):
-                nc.sync.dma_start(
-                    out=h2_sb[t][:, u * 64:(u + 1) * 64, :].rearrange("n (b w) d -> n b (w d)", w=16),
-                    in_=rows[u])
-                if t == 0 and u == 0:
-                    nc.sync.dma_start(out=x_sb[:], in_=x.rearrange("(t n) f d -> n t (f d)", n=P))
+            nc.sync.dma_start(
+                out=h2_sb[t][:, u * 64:(u + 1) * 64, :].rearrange("n (b w) d -> n b (w d)", w=16), in_=rows[u])
 
         def load_x12(t):
             x12_sb[t] = work.tile([P, 2 * G, D], BF16, name="x12_sb", bufs=3)
             nc.sync.dma_start(out=x12_sb[t][:, 0:G, :], in_=x1[t * P:(t + 1) * P])
             nc.sync.dma_start(out=x12_sb[t][:, G:2 * G, :], in_=x2[t * P:(t + 1) * P])
 
-        load_h2(0)
+        load_h2(0, 0)
+        nc.sync.dma_start(out=x_sb[:], in_=x.rearrange("(t n) f d -> n t (f d)", n=P))
+        load_h2(0, 1)
         w_raw = keep.tile([P, 2, F * G], BF16, name="w_raw")
-        nc.sync.dma_start(out=w_raw[:], in_=w3.rearrange("(c o) f g -> o c (f g)", o=P))
+        nc.sync.dma_start(out=w_raw[:], in_=w3.rearrange("(h o) f g -> o h (f g)", o=P))
         load_x12(0)
-        load_h2(1)
+        load_h2(1, 0)
+        load_h2(1, 1)
         ow_raw = keep.tile([P, 4 * NOUT], U8, name="ow_raw")
         nc.sync.dma_start(out=ow_raw[:], in_=out_w_bytes.rearrange("(p j) n -> p (j n)", j=4))
         ow_scale = keep.tile([P, 4], F32, name="ow_scale")
         nc.sync.dma_start(out=ow_scale[:], in_=out_w_scale.rearrange("(p j) o -> p (j o)", j=4))
-        load_h2(2)
+        load_h2(2, 0)
+        load_h2(2, 1)
         load_x12(1)
-        load_h2(3)
+        load_h2(3, 0)
+        load_h2(3, 1)
         load_x12(2)
         b3_row = keep.tile([P, OC], BF16, name="b3_row")
         nc.gpsimd.dma_start(out=b3_row[:], in_=b3.partition_broadcast(P))
@@ -98,84 +100,87 @@ def tile_cin_pb_t_kernel(tc, x, x1, x2, h2, w3, b3, out_w_bytes, out_w_scale, ou
         make_identity(nc, ident_f[:])
         ident_b = keep.tile([P, P], BF16, name="ident_b")
         make_identity(nc, ident_b[:])
-        warm = keep.tile([P, 1], F32, name="warm")
-        nc.vector.memset(warm[:], 0.0)
-        nc.scalar.activation(out=warm[:], in_=warm[:], func=ACT.Relu)
+        table = keep.tile([P, 1], F32, name="table")
+        nc.vector.memset(table[:], 0.0)
+        nc.scalar.activation(out=table[:], in_=table[:], func=ACT.Relu)
 
         x_pair = keep.tile([P, NT, F, D, 2], BF16, name="x_pair")
+        w_perm = keep.tile([P, 2, 2, 16, 16], BF16, name="w_perm")
+        w_q = keep.tile([P, 2 * P * 4], BF16, name="w_q", align_bytes=64)
+        w_codes = keep.tile([P, OC], U32, name="w_codes", align_bytes=64)
+        w_scales = keep.tile([P, OC], U8, name="w_scales", align_bytes=64)
+        b3_col = keep.tile([P, 2], F32, name="b3_col")
+        neg_b3_col = keep.tile([P, 2], F32, name="neg_b3_col")
+        ow_q = keep.tile([P, NOUT, 4], BF16, name="ow_q", align_bytes=64)
+        ow_codes = keep.tile([P, NOUT], U32, name="ow_codes", align_bytes=64)
+        ow_scales = keep.tile([P, NOUT], U8, name="ow_scales", align_bytes=64)
+
+        def add_transpose(dst, data, start, stop):
+            nc.tensor.matmul(dst, lhsT=data, rhs=ident_f[:], is_transpose=True, start=start, stop=stop)
+
+        h2_dg = {}
+        products = {}
+        turned = {}
+        q_in = {}
+        codes = {}
+        scales = {}
+        z = {}
+        y = {}
+        sums = {}
+        pooled_ps = {}
 
         def pair_x():
             nc.vector.tensor_copy(
                 out=x_pair[:].rearrange("n t f d e -> n (t f d) e"),
                 in_=x_sb[:].rearrange("n t k -> n (t k)").unsqueeze(2).to_broadcast([P, NT * F * D, 2]))
 
-        h2r = {}
-        p_sb = {}
-        q_in = {}
-        codes = {}
-        scales = {}
-        tr = {}
-        z = {}
-        y = {}
-        pb = {}
+        def arrange(c, copy, g0=0, g1=G):
+            d0 = c % PER_NT * CD
+            r, i = RUN_OF[c]
+            if r not in h2_dg:
+                h2_dg[r] = work.tile([P, RUN_D, G], BF16, name="h2_dg", bufs=5)
+            copy(out=h2_dg[r][:, i * CD:(i + 1) * CD, g0:g1].rearrange("n i g -> n g i"),
+                 in_=h2_sb[c // PER_NT][:, g0:g1, d0:d0 + CD])
 
-        def arrange(c, eng, g0=0, g1=G):
-            t, d0 = c // PER_NT, c % PER_NT * CD
-            g, b = GROUP_OF[c]
-            if g not in h2r:
-                h2r[g] = work.tile([P, 4 * CD, G], BF16, name="h2r", bufs=5)
-            dst = h2r[g][:, b * CD:b * CD + CD, g0:g1].rearrange("n i g -> n g i")
-            src = h2_sb[t][:, g0:g1, d0:d0 + 4]
-            if eng == 0:
-                nc.vector.tensor_copy(out=dst, in_=src)
-            else:
-                nc.scalar.copy(out=dst, in_=src)
+        def product(r, f):
+            c, size = RUNS[r]
+            d0, nd = c % PER_NT * CD, size * CD
+            if r not in products:
+                products[r] = work.tile([P, RUN_D, 2, F, 64], BF16, name="products", bufs=3)
+            nc.vector.tensor_tensor(
+                out=products[r][:, 0:nd, :, f, :],
+                in0=h2_dg[r][:, 0:nd, :].rearrange("n d (u k) -> n d u k", u=2),
+                in1=x_pair[:, c // PER_NT, f, d0:d0 + nd, :].unsqueeze(2).to_broadcast([P, nd, 64, 2]),
+                op=ALU.mult)
 
-        def product(g, f):
-            c, n = GROUPS[g]
-            t, dg = c // PER_NT, c % PER_NT * CD
-            d0, nd = 0, n * CD
-            if g not in p_sb:
-                p_sb[g] = work.tile([P, 4 * CD, 2, F, 64], BF16, name="p_sb", bufs=3)
-            if True:
-                nc.vector.tensor_tensor(
-                    out=p_sb[g][:, d0:d0 + nd, :, f, :],
-                    in0=h2r[g][:, d0:d0 + nd, :].rearrange("n d (u k) -> n d u k", u=2),
-                    in1=x_pair[:, t, f, dg + d0:dg + d0 + nd, :].unsqueeze(2).to_broadcast([P, nd, 64, 2]),
-                    op=ALU.mult)
-
-        def transposes(c):
-            g, b = GROUP_OF[c]
-            words = p_sb[g][:].rearrange("n d u f w -> n (d u f w)").bitcast(F32)
-            for h in range(2):
-                tr[c, h] = ps.tile([P, 2, 2, P], F32, name="tr", bufs=3)
-                for i in range(2):
+        def transpose_chunk(c):
+            r, i = RUN_OF[c]
+            words = products[r][:].rearrange("n d u f k -> n (d u f k)").bitcast(F32)
+            for half in range(2):
+                turned[c, half] = ps.tile([P, 2, 2, P], F32, name="tr", bufs=3)
+                for dd in range(2):
                     for u in range(2):
-                        w0 = ((b * CD + h * 2 + i) * 2 + u) * P
-                        nc.tensor.transpose(tr[c, h][:, i, u, :], words[:, w0:w0 + P], ident_f[:])
+                        w0 = ((i * CD + half * 2 + dd) * 2 + u) * P
+                        nc.tensor.transpose(turned[c, half][:, dd, u, :], words[:, w0:w0 + P], ident_f[:])
 
-        def empty(c, h):
-            if h == 0:
-                q_in[c] = work.tile([P, CD * P * 4], BF16, name="q_in", bufs=3, align_bytes=64)
+        def unload(c, half, copy):
+            if half == 0:
+                q_in[c] = work.tile([P, COLS * 4], BF16, name="q_in", bufs=3, align_bytes=64)
             words = q_in[c][:].bitcast(F32)
-            dst = words[:, h * 512:(h + 1) * 512].rearrange("p (d n u) -> p d n u", d=2, u=2)
-            src = tr[c, h][:].rearrange("p d u n -> p d n u")
-            if (c, h) in EV_ON_V:
-                nc.vector.tensor_copy(out=dst, in_=src)
-            else:
-                nc.scalar.copy(out=dst, in_=src)
+            copy(out=words[:, half * COLS:(half + 1) * COLS].rearrange("p (d n u) -> p d n u", d=2, u=2),
+                 in_=turned[c, half][:].rearrange("p d u n -> p d n u"))
 
         def quantize(c):
-            codes[c] = work.tile([P, CD * P], U32, name="codes", bufs=4, align_bytes=64)
-            scales[c] = work.tile([P, CD * P], U8, name="scales", bufs=4, align_bytes=64)
+            codes[c] = work.tile([P, COLS], U32, name="codes", bufs=4, align_bytes=64)
+            scales[c] = work.tile([P, COLS], U8, name="scales", bufs=4, align_bytes=64)
             nc.vector.quantize_mx(out=codes[c][:].bitcast(FP8X4), scales=scales[c][:], in_=q_in[c][:])
 
         def layer(c):
             for o in range(2):
                 if c >= Z_IN_TR:
-                    z[c, o] = ps.tile([P, CD * P], F32, name="tr", bufs=3)
+                    z[c, o] = ps.tile([P, COLS], F32, name="tr", bufs=3)
                 else:
-                    z[c, o] = ps.tile([P, CD * P], F32, name="z", bufs=3)
+                    z[c, o] = ps.tile([P, COLS], F32, name="z", bufs=2)
                 nc.tensor.matmul_mx(
                     out=z[c, o][:],
                     lhsT=w_codes[:, o * P:(o + 1) * P].bitcast(FP8X4), lhsT_scale=w_scales[:, o * P:(o + 1) * P],
@@ -183,235 +188,259 @@ def tile_cin_pb_t_kernel(tc, x, x1, x2, h2, w3, b3, out_w_bytes, out_w_scale, ou
 
         def relu(c, o):
             if o == 0:
-                y[c] = work.tile([P, 2, CD * P], F32, name="y", bufs=4)
-            w = CD * P // 2 if (c, o) in PAIRED else CD * P
-            nc.scalar.activation(out=y[c][:, o, 0:w], in_=z[c, o][:, 0:w], func=ACT.Relu, bias=b3_col[:, o:o + 1])
+                y[c] = work.tile([P, 2, COLS], F32, name="y", bufs=4)
+            if (c, o) not in ON_VECTOR:
+                w = COLS // 2 if (c, o) in PAIRED else COLS
+                nc.scalar.activation(
+                    out=y[c][:, o, 0:w], in_=z[c, o][:, 0:w], func=ACT.Relu, bias=b3_col[:, o:o + 1])
 
-        def relu_pair(c, o):
+        def relu_on_vector(c, o):
+            neg_b = neg_b3_col[:, o:o + 1]
+            t = c // PER_NT
+            if (c, o) in ON_VECTOR:
+                if (t, o) not in sums:
+                    sums[t, o] = work.tile([P, COLS], F32, name="sums", bufs=4)
+                    nc.vector.tensor_scalar(
+                        out=sums[t, o][:], in0=z[c, o][:], scalar1=neg_b, scalar2=None, op0=ALU.max)
+                else:
+                    nc.vector.scalar_tensor_tensor(
+                        out=sums[t, o][:], in0=z[c, o][:], scalar=neg_b, in1=sums[t, o][:],
+                        op0=ALU.max, op1=ALU.add)
             if (c, o) in PAIRED:
-                h = CD * P // 2
+                w = COLS // 2
                 nc.vector.scalar_tensor_tensor(
-                    out=y[c][:, o, h:2 * h], in0=z[c, o][:, h:2 * h], scalar=nb3_col[:, o:o + 1],
-                    in1=y[c][:, o, 0:h], op0=ALU.max, op1=ALU.add)
+                    out=y[c][:, o, w:COLS], in0=z[c, o][:, w:COLS], scalar=neg_b, in1=y[c][:, o, 0:w],
+                    op0=ALU.max, op1=ALU.add)
 
         def pool(c):
-            t = c // PER_NT
+            t, last = c // PER_NT, c % PER_NT == PER_NT - 1
             if c % PER_NT == 0:
-                pb[t] = ps.tile([P, FINAL], F32, name="pb", bufs=1)
+                pooled_ps[t] = ps.tile([P, FINAL], F32, name="pooled_ps", bufs=1)
+            blocks = []
             for o in range(2):
-                i0 = CD // 2 if (c, o) in PAIRED else 0
-                for i in range(i0, CD):
-                    nc.tensor.matmul(
-                        pb[t][:, 2 * G + o * P:2 * G + (o + 1) * P],
-                        lhsT=y[c][:, o, i * P:(i + 1) * P], rhs=ident_f[:], is_transpose=True,
-                        start=(c % PER_NT == 0 and o == 0 and i == i0),
-                        stop=(c % PER_NT == PER_NT - 1 and o == 1 and i == CD - 1))
+                if last and (t, o) in sums:
+                    blocks.extend([(o, sums[t, o][:, i * P:(i + 1) * P]) for i in range(CD)])
+            for o in range(2):
+                if (c, o) not in ON_VECTOR:
+                    first = CD // 2 if (c, o) in PAIRED else 0
+                    blocks.extend([(o, y[c][:, o, i * P:(i + 1) * P]) for i in range(first, CD)])
+            for i, (o, data) in enumerate(blocks):
+                add_transpose(pooled_ps[t][:, 2 * G + o * P:2 * G + (o + 1) * P], data,
+                              start=(c % PER_NT == 0 and i == 0), stop=(last and i == len(blocks) - 1))
 
-        xr = {}
-        xr_sb = {}
-        xp = {}
+        plain_ps = {}
+        plain_sb = {}
+        rest_ps = {}
+        rest_sb = {}
+        pair_sums = {}
 
         def x_plain(t, i):
-            for d in (2 * i, 2 * i + 1):
-                nc.tensor.matmul(pb[t][:, 0:2 * G], lhsT=ident_b[:], rhs=x12_sb[t][:, :, d], start=False, stop=False)
+            if i == 0:
+                plain_ps[t] = ps.tile([P, 2 * G, 2], F32, name="plain_ps", bufs=1)
+            nc.tensor.matmul(plain_ps[t][:], lhsT=ident_b[:], rhs=x12_sb[t][:, :, 2 * i:2 * i + 2],
+                             start=(i == 0), stop=(i == PLAIN_D // 2 - 1))
+
+        def x_plain_out(t):
+            plain_sb[t] = work.tile([P, 2 * G], F32, name="plain_sb", bufs=2)
+            nc.vector.tensor_reduce(
+                out=plain_sb[t][:], in_=plain_ps[t][:], axis=mybir.AxisListType.X, op=ALU.add)
 
         def x_pairs(t, k):
             if k == 0:
-                xp[t] = work.tile([P, PAIRS, 2 * G], F32, name="xp", bufs=2)
+                pair_sums[t] = work.tile([P, PAIRS, 2 * G], F32, name="pair_sums", bufs=2)
             i0, n, c0, c1 = PIECES[k]
-            a = PLAIN_D + i0
+            d0 = PLAIN_D + i0
             nc.vector.tensor_tensor(
-                out=xp[t][:, i0:i0 + n, c0:c1].rearrange("n i c -> n c i"),
-                in0=x12_sb[t][:, c0:c1, a:a + n],
-                in1=x12_sb[t][:, c0:c1, a + PAIRS:a + PAIRS + n], op=ALU.add)
+                out=pair_sums[t][:, i0:i0 + n, c0:c1].rearrange("n i c -> n c i"),
+                in0=x12_sb[t][:, c0:c1, d0:d0 + n], in1=x12_sb[t][:, c0:c1, d0 + PAIRS:d0 + PAIRS + n], op=ALU.add)
 
         def x_rest(t, k):
             i0, n, c0, c1 = PIECES[k]
-            if (i0, c0) == (0, 0):
-                xr[t] = ps.tile([P, 2, P], F32, name="xr", bufs=1)
+            if k == 0:
+                rest_ps[t] = ps.tile([P, 2, P], F32, name="rest_ps", bufs=1)
             for o in range(c0 // G, c1 // G):
                 for i in range(i0, i0 + n):
-                    nc.tensor.matmul(
-                        xr[t][:, o, :], lhsT=xp[t][:, i, o * P:(o + 1) * P], rhs=ident_f[:], is_transpose=True,
-                        start=(o == 0 and i == 0), stop=(o == 1 and i == PAIRS - 1))
+                    add_transpose(rest_ps[t][:, o, :], pair_sums[t][:, i, o * P:(o + 1) * P],
+                                  start=(o == 0 and i == 0), stop=(o == 1 and i == PAIRS - 1))
 
         def x_rest_out(t):
-            xr_sb[t] = work.tile([P, 2, P], F32, name="xr_sb", bufs=2)
-            nc.scalar.copy(out=xr_sb[t][:], in_=xr[t][:])
+            rest_sb[t] = work.tile([P, 2, P], F32, name="rest_sb", bufs=2)
+            nc.scalar.copy(out=rest_sb[t][:], in_=rest_ps[t][:])
 
         def x_rest_back(t):
             for o in range(2):
-                nc.tensor.matmul(pb[t][:, o * P:(o + 1) * P], lhsT=xr_sb[t][:, o, :], rhs=ident_f[:],
-                                 is_transpose=True, start=False, stop=False)
+                add_transpose(pooled_ps[t][:, o * P:(o + 1) * P], rest_sb[t][:, o, :], start=False, stop=False)
 
         pooled = {}
-        ftr = {}
-        fq = {}
-        fcodes = {}
-        fscales = {}
+        pooled_turned = {}
+        pooled_q = {}
+        pooled_codes = {}
+        pooled_scales = {}
+        out_ps = {}
 
-        def fin_pool(t):
+        def finish_pooled(t):
             pooled[t] = work.tile([P, FINAL], BF16, name="pooled", bufs=2)
-            nc.vector.tensor_copy(out=pooled[t][:, 0:2 * G], in_=pb[t][:, 0:2 * G])
+            nc.vector.tensor_tensor(
+                out=pooled[t][:, 0:2 * G], in0=pooled_ps[t][:, 0:2 * G], in1=plain_sb[t][:], op=ALU.add)
             for o in range(2):
-                left = sum([CD // 2 for c, oo in PAIRED if c // PER_NT == t and oo == o])
+                missing = sum([CD // 2 for c, half in PAIRED if c // PER_NT == t and half == o])
+                missing = missing + sum([CD for c, half in ON_VECTOR if c // PER_NT == t and half == o])
                 cols = slice(2 * G + o * P, 2 * G + (o + 1) * P)
-                if left:
+                if missing:
                     nc.vector.scalar_tensor_tensor(
-                        out=pooled[t][:, cols], in0=b3_row[:, o * P:(o + 1) * P], scalar=float(left),
-                        in1=pb[t][:, cols], op0=ALU.mult, op1=ALU.add)
+                        out=pooled[t][:, cols], in0=b3_row[:, o * P:(o + 1) * P], scalar=float(missing),
+                        in1=pooled_ps[t][:, cols], op0=ALU.mult, op1=ALU.add)
                 else:
-                    nc.scalar.copy(out=pooled[t][:, cols], in_=pb[t][:, cols])
+                    nc.scalar.copy(out=pooled[t][:, cols], in_=pooled_ps[t][:, cols])
 
-        def fin_transpose(t):
+        def finish_transpose(t):
             words = pooled[t][:].bitcast(F32)
-            ftr[t] = ps.tile([P, 2, P], F32, name="tr", bufs=3)
+            pooled_turned[t] = ps.tile([P, 2, P], F32, name="tr", bufs=3)
             for u in range(2):
-                nc.tensor.transpose(ftr[t][:, u, :], words[:, u:FINAL // 2:2], ident_f[:])
+                nc.tensor.transpose(pooled_turned[t][:, u, :], words[:, u:FINAL // 2:2], ident_f[:])
 
-        def fin_empty(t):
-            fq[t] = work.tile([P, 4 * P], BF16, name="fq", bufs=2, align_bytes=64)
-            nc.scalar.copy(out=fq[t][:].bitcast(F32).rearrange("p (n u) -> p n u", u=2),
-                           in_=ftr[t][:].rearrange("p u n -> p n u"))
+        def finish_unload(t):
+            pooled_q[t] = work.tile([P, 4 * P], BF16, name="pooled_q", bufs=2, align_bytes=64)
+            nc.scalar.copy(out=pooled_q[t][:].bitcast(F32).rearrange("p (n u) -> p n u", u=2),
+                           in_=pooled_turned[t][:].rearrange("p u n -> p n u"))
 
-        def fin_quantize(t):
-            fcodes[t] = work.tile([P, P], U32, name="fcodes", bufs=2, align_bytes=64)
-            fscales[t] = work.tile([P, P], U8, name="fscales", bufs=2, align_bytes=64)
-            nc.vector.quantize_mx(out=fcodes[t][:].bitcast(FP8X4), scales=fscales[t][:], in_=fq[t][:])
+        def finish_quantize(t):
+            pooled_codes[t] = work.tile([P, P], U32, name="pooled_codes", bufs=2, align_bytes=64)
+            pooled_scales[t] = work.tile([P, P], U8, name="pooled_scales", bufs=2, align_bytes=64)
+            nc.vector.quantize_mx(
+                out=pooled_codes[t][:].bitcast(FP8X4), scales=pooled_scales[t][:], in_=pooled_q[t][:])
 
-        facc = {}
+        def finish_matmul(t):
+            out_ps[t] = ps.tile([P, NOUT], F32, name="tr", bufs=3)
+            nc.tensor.matmul_mx(
+                out=out_ps[t][:], lhsT=pooled_codes[t][:].bitcast(FP8X4), lhsT_scale=pooled_scales[t][:],
+                rhs=ow_codes[:].bitcast(FP8X4), rhs_scale=ow_scales[:], start=True, stop=True)
 
-        def fin_mm(t):
-            facc[t] = ps.tile([P, NOUT], F32, name="z", bufs=3)
-            nc.tensor.matmul_mx(out=facc[t][:], lhsT=fcodes[t][:].bitcast(FP8X4), lhsT_scale=fscales[t][:],
-                                rhs=ow_codes[:].bitcast(FP8X4), rhs_scale=ow_scales[:], start=True, stop=True)
+        def finish_store(t):
+            result = work.tile([P, NOUT], F32, name="result", bufs=2)
+            nc.vector.tensor_tensor(out=result[:], in0=out_ps[t][:], in1=ob_row[:], op=ALU.add)
+            nc.sync.dma_start(out=out[t * P:(t + 1) * P, :], in_=result[:])
 
-        def fin_out(t):
-            res = work.tile([P, NOUT], F32, name="res", bufs=2)
-            nc.vector.tensor_tensor(out=res[:], in0=facc[t][:], in1=ob_row[:], op=ALU.add)
-            nc.sync.dma_start(out=out[t * P:(t + 1) * P, :], in_=res[:])
+        def prepare_out_w():
+            for j in range(4):
+                nc.vector.tensor_scalar(
+                    out=ow_q[:, :, j], in0=ow_raw[:, j * NOUT:(j + 1) * NOUT].bitcast(FP8),
+                    scalar1=ow_scale[:, j:j + 1], scalar2=None, op0=ALU.mult)
+            nc.vector.quantize_mx(out=ow_codes[:].bitcast(FP8X4), scales=ow_scales[:],
+                                  in_=ow_q[:].rearrange("p n j -> p (n j)"))
 
-        arrange(0, 0, 0, G // 2)
+        arrange(0, nc.vector.tensor_copy, 0, G // 2)
         pair_x()
-        for c in range(1, HALF_ON_V + 1):
-            arrange(c, 0, 0, G // 2)
-        arrange(0, 0, G // 2, G)
-        arrange(1, 1, G // 2 if HALF_ON_V >= 1 else 0)
+        arrange(0, nc.vector.tensor_copy, G // 2, G)
+        arrange(1, nc.scalar.copy)
         for f in range(F):
             product(0, f)
-        w_perm = keep.tile([P, 2, 2, 16, 16], BF16, name="w_perm")
-        transposes(0)
-        arrange(2, 1, G // 2 if HALF_ON_V >= 2 else 0)
-        arrange(3, 1, G // 2 if HALF_ON_V >= 3 else 0)
-        empty(0, 0)
-        empty(0, 1)
+        transpose_chunk(0)
+        arrange(2, nc.scalar.copy)
+        arrange(3, nc.scalar.copy)
+        unload(0, 0, nc.scalar.copy)
+        unload(0, 1, nc.scalar.copy)
         for f in range(F):
             product(1, f)
+
         for u in range(2):
             nc.vector.tensor_copy(out=w_perm[:, :, u, :, :],
-                                  in_=w_raw[:].rearrange("o c (b u w) -> o u c b w", u=2, w=16)[:, u])
-        b3_ps = ps.tile([P, 2, P], BF16, name="xr", bufs=1)
+                                  in_=w_raw[:].rearrange("o h (q u w) -> o u h q w", u=2, w=16)[:, u])
+        b3_ps = ps.tile([P, 2, P], BF16, name="rest_ps", bufs=1)
         for o in range(2):
             nc.tensor.transpose(b3_ps[:, o, :], b3_row[:, o * P:(o + 1) * P], ident_b[:])
-        w_tr = ps.tile([P, 2, 2, P], F32, name="tr", bufs=3)
-        w_words = w_perm[:].rearrange("o c u b w -> o (c u b w)").bitcast(F32)
+        w_turned = ps.tile([P, 2, 2, P], F32, name="tr", bufs=3)
+        w_words = w_perm[:].rearrange("o h u q w -> o (h u q w)").bitcast(F32)
         for o in range(2):
             for u in range(2):
-                nc.tensor.transpose(w_tr[:, o, u, :], w_words[:, (2 * o + u) * P:(2 * o + u + 1) * P], ident_f[:])
-        w_q = keep.tile([P, 2 * P * 4], BF16, name="w_q", align_bytes=64)
-        nc.scalar.copy(out=w_q[:].bitcast(F32).rearrange("p (c o u) -> p c o u", c=2, u=2),
-                       in_=w_tr[:].rearrange("p c u o -> p c o u"))
-        b3_col = keep.tile([P, 2], F32, name="b3_col")
+                nc.tensor.transpose(
+                    w_turned[:, o, u, :], w_words[:, (2 * o + u) * P:(2 * o + u + 1) * P], ident_f[:])
+        nc.scalar.copy(out=w_q[:].bitcast(F32).rearrange("p (h o u) -> p h o u", h=2, u=2),
+                       in_=w_turned[:].rearrange("p h u o -> p h o u"))
         nc.scalar.copy(out=b3_col[:], in_=b3_ps[:, :, 0])
         for f in range(F):
             product(2, f)
             if f == 1:
                 quantize(0)
-        w_codes = keep.tile([P, OC], U32, name="w_codes", align_bytes=64)
-        w_scales = keep.tile([P, OC], U8, name="w_scales", align_bytes=64)
         nc.vector.quantize_mx(out=w_codes[:].bitcast(FP8X4), scales=w_scales[:], in_=w_q[:])
-        for c in range(4, A_AHEAD + 1):
-            arrange(c, 1 if c in ARR_S else 0)
-        for st, g, f in PRODUCTS:
-            if st <= 0 and g > 2:
-                product(g, f)
+        arrange(4, nc.scalar.copy)
+        for c in range(5, ARRANGE_AHEAD + 1):
+            arrange(c, nc.vector.tensor_copy)
 
-        nb3_col = keep.tile([P, 2], F32, name="nb3_col")
-        ow_q = keep.tile([P, NOUT, 4], BF16, name="ow_q", align_bytes=64)
-        ow_codes = keep.tile([P, NOUT], U32, name="ow_codes", align_bytes=64)
-        ow_scales = keep.tile([P, NOUT], U8, name="ow_scales", align_bytes=64)
+        for s in range(1, CHUNKS + 6):
+            tiles = [(t, s - PER_NT * t, FINISH_LAST if t == NT - 1 else FINISH) for t in range(NT)]
+            c_relu = s - RELU if 0 <= s - RELU < CHUNKS else None
 
-        for s in range(1, CHUNKS + 8):
-            places = [(t, s - PER_NT * t, O_LAST if t == NT - 1 else O_FIN) for t in range(NT)]
-            for t, o, fin in places:
-                if o == fin[0]:
-                    fin_pool(t)
-            if 0 <= s - LR < CHUNKS:
-                relu(s - LR, 0)
+            for t, at, finish in tiles:
+                if at == finish[0]:
+                    finish_pooled(t)
+            if c_relu is not None:
+                relu(c_relu, 0)
             if s < CHUNKS:
-                transposes(s)
-                empty(s, 0)
-            if 0 <= s - LR < CHUNKS:
-                relu(s - LR, 1)
-            if s < CHUNKS and (s, 1) not in EV_ON_V:
-                empty(s, 1)
-            for t, o, fin in places:
-                if o == O_REST_OUT[t]:
+                transpose_chunk(s)
+                unload(s, 0, nc.scalar.copy)
+            if c_relu is not None:
+                relu(c_relu, 1)
+            if s < CHUNKS - 1:
+                unload(s, 1, nc.scalar.copy)
+            for t, at, finish in tiles:
+                if at == X_REST_OUT[t]:
                     x_rest_out(t)
-            if s == PER_NT + 4:
-                load_x12(3)
-            for t, o, fin in places:
-                if o == fin[4] + 1 and t < NT - 1:
-                    fin_out(t)
-            for st, g, f in PRODUCTS:
-                if st == s:
-                    product(g, f)
-            if 1 <= s - LQ < CHUNKS:
-                quantize(s - LQ)
-            if (s, 1) in EV_ON_V:
-                empty(s, 1)
-            for o in range(2):
-                if 0 <= s - LR < CHUNKS:
-                    relu_pair(s - LR, o)
-            if s + A_AHEAD < CHUNKS:
-                arrange(s + A_AHEAD, 1 if s + A_AHEAD in ARR_S else 0)
-            for t, o, fin in places:
-                for k in range(5):
-                    if o == O_PAIR[t][k]:
+            if s == X12_STEP:
+                load_x12(NT - 1)
+
+            for t, at, finish in tiles:
+                if at == finish[4] + 1 and t < NT - 1:
+                    finish_store(t)
+            for step, r, f in PRODUCTS:
+                if step == s:
+                    product(r, f)
+            if 1 <= s - QUANTIZE < CHUNKS:
+                quantize(s - QUANTIZE)
+            if s == CHUNKS - 1:
+                unload(s, 1, nc.vector.tensor_copy)
+            if c_relu is not None:
+                relu_on_vector(c_relu, 0)
+                relu_on_vector(c_relu, 1)
+            if s + ARRANGE_AHEAD < CHUNKS:
+                arrange(s + ARRANGE_AHEAD, nc.vector.tensor_copy)
+            for t, at, finish in tiles:
+                for k in range(len(PIECES)):
+                    if at == X_PAIRS[t][k]:
                         x_pairs(t, k)
-                if o == fin[3]:
-                    fin_quantize(t)
-            if s == 2:
-                nc.vector.tensor_scalar(out=nb3_col[:], in0=b3_col[:], scalar1=-1.0, scalar2=None, op0=ALU.mult)
-            if s == S_OW:
-                for j in range(4):
-                    nc.vector.tensor_scalar(
-                        out=ow_q[:, :, j], in0=ow_raw[:, j * NOUT:(j + 1) * NOUT].bitcast(FP8),
-                        scalar1=ow_scale[:, j:j + 1], scalar2=None, op0=ALU.mult)
-                nc.vector.quantize_mx(out=ow_codes[:].bitcast(FP8X4), scales=ow_scales[:],
-                                      in_=ow_q[:].rearrange("p n j -> p (n j)"))
-            for t, o, fin in places:
-                if o == fin[1]:
-                    fin_transpose(t)
-                if o == O_REST_BACK[t]:
+                if at == X_PLAIN_OUT[t]:
+                    x_plain_out(t)
+                if at == finish[3]:
+                    finish_quantize(t)
+            if s == LAYER:
+                nc.vector.tensor_scalar(
+                    out=neg_b3_col[:], in0=b3_col[:], scalar1=-1.0, scalar2=None, op0=ALU.mult)
+            if s == OUT_W_STEP:
+                prepare_out_w()
+
+            for t, at, finish in tiles:
+                if at == finish[1]:
+                    finish_transpose(t)
+                if at == X_REST_BACK[t]:
                     x_rest_back(t)
-            if s >= CHUNKS and 0 <= s - LM < CHUNKS:
-                layer(s - LM)
-            if 0 <= s - LW < CHUNKS:
-                pool(s - LW)
-            for t, o, fin in places:
-                for k in range(5):
-                    if o == O_REST[t][k]:
+            if CHUNKS <= s < CHUNKS + LAYER:
+                layer(s - LAYER)
+            if 0 <= s - POOL < CHUNKS:
+                pool(s - POOL)
+            for t, at, finish in tiles:
+                for k in range(len(PIECES)):
+                    if at == X_REST[t][k]:
                         x_rest(t, k)
-                for i in range(6):
-                    if o == O_PLAIN[t][i]:
+            for t, at, finish in tiles:
+                for i in range(PLAIN_D // 2):
+                    if at == X_PLAIN[t][i]:
                         x_plain(t, i)
-            if s < CHUNKS and 0 <= s - LM < CHUNKS:
-                layer(s - LM)
-            for t, o, fin in places:
-                if o == fin[2]:
-                    fin_empty(t)
-                if o == fin[4]:
-                    fin_mm(t)
+            if LAYER <= s < CHUNKS:
+                layer(s - LAYER)
+            for t, at, finish in tiles:
+                if at == finish[2]:
+                    finish_unload(t)
+                if at == finish[4]:
+                    finish_matmul(t)
                     if t == NT - 1:
-                        fin_out(t)
+                        finish_store(t)

from contextlib import ExitStack

import concourse.mybir as mybir
from concourse.masks import make_identity

F32 = mybir.dt.float32
BF16 = mybir.dt.bfloat16
U32 = mybir.dt.uint32
U8 = mybir.dt.uint8
FP8 = mybir.dt.float8_e4m3fn
FP8X4 = mybir.dt.float8_e4m3fn_x4
ALU = mybir.AluOpType
ACT = mybir.ActivationFunctionType

B, F, D, G, OC = 512, 4, 32, 128, 256
FINAL, NOUT = 512, 128
P = 128
FLOPS = 2 * B * D * F * G * OC + 2 * B * FINAL * NOUT

NT = B // P
CD = 4
COLS = CD * P
PER_NT = D // CD
CHUNKS = NT * PER_NT

SIZES = [1, 1, 2, 2, 2] + [4] * 6
RUNS = [(sum(SIZES[:r]), size) for r, size in enumerate(SIZES)]
RUN_OF = {c + i: (r, i) for r, (c, size) in enumerate(RUNS) for i in range(size)}
RUN_D = 4 * CD
PRODUCTS = [(c - size + f * size // F, r, f) for r, (c, size) in enumerate(RUNS) for f in range(F)]

PLAIN_D = 12
PAIRS = (D - PLAIN_D) // 2
PIECES = ((0, 4, 0, G), (0, 4, G, 2 * G), (4, 4, 0, G), (4, 4, G, 2 * G), (8, 2, 0, 2 * G))

ON_VECTOR = [(c, 1) for c in (3, 11, 19, 25, 26, 27, 29)]
PAIRED = [(c, 0) for c in (23, 24, 25, 26, 29, 31)] + [(30, 1)]

QUANTIZE, LAYER, RELU, POOL = 1, 2, 3, 4
X_PAIRS = ((3, 4, 6, 6, 8), (1, 3, 4, 4, 6), (1, 2, 4, 6, 6), (-2, 2, 3, 4, 5))
X_REST = ((4, 6, 7, 8, 9), (3, 5, 6, 8, 8), (3, 3, 7, 8, 8), (2, 4, 4, 5, 7))
X_REST_OUT = (10, 10, 9, 9)
X_REST_BACK = (11, 11, 10, 11)
X_PLAIN = ((2, 3, 4, 5, 5, 7), (2, 3, 4, 6, 6, 6), (2, 2, 4, 5, 7, 7), (1, 2, 3, 5, 5, 6))
X_PLAIN_OUT = (8, 9, 8, 7)
FINISH = (12, 13, 13, 14, 14)
FINISH_LAST = (12, 12, 12, 13, 13)
ARRANGE_AHEAD = 8
X12_STEP = 12
OUT_W_STEP = 12
Z_IN_TR = CHUNKS - 2


def tile_cin_pb_t_kernel(tc, x, x1, x2, h2, w3, b3, out_w_bytes, out_w_scale, out_b, out):
    nc = tc.nc
    with ExitStack() as ctx:
        keep = ctx.enter_context(tc.tile_pool(name="keep", bufs=1))
        work = ctx.enter_context(tc.tile_pool(name="work", bufs=3))
        ps = ctx.enter_context(tc.psum_pool(name="ps", bufs=1))
        ctx.enter_context(tc.manual_schedule())

        x_sb = keep.tile([P, NT, F * D], BF16, name="x_sb")
        h2_sb = [work.tile([P, G, D], BF16, name="h2_sb", bufs=NT) for t in range(NT)]
        x12_sb = {}

        def load_h2(t, u):
            rows = h2[t * P:(t + 1) * P].rearrange("n (b u w) d -> u n b (w d)", u=2, w=16)
            nc.sync.dma_start(
                out=h2_sb[t][:, u * 64:(u + 1) * 64, :].rearrange("n (b w) d -> n b (w d)", w=16), in_=rows[u])

        def load_x12(t):
            x12_sb[t] = work.tile([P, 2 * G, D], BF16, name="x12_sb", bufs=3)
            nc.sync.dma_start(out=x12_sb[t][:, 0:G, :], in_=x1[t * P:(t + 1) * P])
            nc.sync.dma_start(out=x12_sb[t][:, G:2 * G, :], in_=x2[t * P:(t + 1) * P])

        load_h2(0, 0)
        nc.sync.dma_start(out=x_sb[:], in_=x.rearrange("(t n) f d -> n t (f d)", n=P))
        load_h2(0, 1)
        w_raw = keep.tile([P, 2, F * G], BF16, name="w_raw")
        nc.sync.dma_start(out=w_raw[:], in_=w3.rearrange("(h o) f g -> o h (f g)", o=P))
        load_x12(0)
        load_h2(1, 0)
        load_h2(1, 1)
        ow_raw = keep.tile([P, 4 * NOUT], U8, name="ow_raw")
        nc.sync.dma_start(out=ow_raw[:], in_=out_w_bytes.rearrange("(p j) n -> p (j n)", j=4))
        ow_scale = keep.tile([P, 4], F32, name="ow_scale")
        nc.sync.dma_start(out=ow_scale[:], in_=out_w_scale.rearrange("(p j) o -> p (j o)", j=4))
        load_h2(2, 0)
        load_h2(2, 1)
        load_x12(1)
        load_h2(3, 0)
        load_h2(3, 1)
        load_x12(2)
        b3_row = keep.tile([P, OC], BF16, name="b3_row")
        nc.gpsimd.dma_start(out=b3_row[:], in_=b3.partition_broadcast(P))
        ob_row = keep.tile([P, NOUT], BF16, name="ob_row")
        nc.gpsimd.dma_start(out=ob_row[:], in_=out_b.partition_broadcast(P))

        ident_f = keep.tile([P, P], F32, name="ident_f")
        make_identity(nc, ident_f[:])
        ident_b = keep.tile([P, P], BF16, name="ident_b")
        make_identity(nc, ident_b[:])
        table = keep.tile([P, 1], F32, name="table")
        nc.vector.memset(table[:], 0.0)
        nc.scalar.activation(out=table[:], in_=table[:], func=ACT.Relu)

        x_pair = keep.tile([P, NT, F, D, 2], BF16, name="x_pair")
        w_perm = keep.tile([P, 2, 2, 16, 16], BF16, name="w_perm")
        w_q = keep.tile([P, 2 * P * 4], BF16, name="w_q", align_bytes=64)
        w_codes = keep.tile([P, OC], U32, name="w_codes", align_bytes=64)
        w_scales = keep.tile([P, OC], U8, name="w_scales", align_bytes=64)
        b3_col = keep.tile([P, 2], F32, name="b3_col")
        neg_b3_col = keep.tile([P, 2], F32, name="neg_b3_col")
        ow_q = keep.tile([P, NOUT, 4], BF16, name="ow_q", align_bytes=64)
        ow_codes = keep.tile([P, NOUT], U32, name="ow_codes", align_bytes=64)
        ow_scales = keep.tile([P, NOUT], U8, name="ow_scales", align_bytes=64)

        def add_transpose(dst, data, start, stop):
            nc.tensor.matmul(dst, lhsT=data, rhs=ident_f[:], is_transpose=True, start=start, stop=stop)

        h2_dg = {}
        products = {}
        turned = {}
        q_in = {}
        codes = {}
        scales = {}
        z = {}
        y = {}
        sums = {}
        pooled_ps = {}

        def pair_x():
            nc.vector.tensor_copy(
                out=x_pair[:].rearrange("n t f d e -> n (t f d) e"),
                in_=x_sb[:].rearrange("n t k -> n (t k)").unsqueeze(2).to_broadcast([P, NT * F * D, 2]))

        def arrange(c, copy, g0=0, g1=G):
            d0 = c % PER_NT * CD
            r, i = RUN_OF[c]
            if r not in h2_dg:
                h2_dg[r] = work.tile([P, RUN_D, G], BF16, name="h2_dg", bufs=5)
            copy(out=h2_dg[r][:, i * CD:(i + 1) * CD, g0:g1].rearrange("n i g -> n g i"),
                 in_=h2_sb[c // PER_NT][:, g0:g1, d0:d0 + CD])

        def product(r, f):
            c, size = RUNS[r]
            d0, nd = c % PER_NT * CD, size * CD
            if r not in products:
                products[r] = work.tile([P, RUN_D, 2, F, 64], BF16, name="products", bufs=3)
            nc.vector.tensor_tensor(
                out=products[r][:, 0:nd, :, f, :],
                in0=h2_dg[r][:, 0:nd, :].rearrange("n d (u k) -> n d u k", u=2),
                in1=x_pair[:, c // PER_NT, f, d0:d0 + nd, :].unsqueeze(2).to_broadcast([P, nd, 64, 2]),
                op=ALU.mult)

        def transpose_chunk(c):
            r, i = RUN_OF[c]
            words = products[r][:].rearrange("n d u f k -> n (d u f k)").bitcast(F32)
            for half in range(2):
                turned[c, half] = ps.tile([P, 2, 2, P], F32, name="tr", bufs=3)
                for dd in range(2):
                    for u in range(2):
                        w0 = ((i * CD + half * 2 + dd) * 2 + u) * P
                        nc.tensor.transpose(turned[c, half][:, dd, u, :], words[:, w0:w0 + P], ident_f[:])

        def unload(c, half, copy):
            if half == 0:
                q_in[c] = work.tile([P, COLS * 4], BF16, name="q_in", bufs=3, align_bytes=64)
            words = q_in[c][:].bitcast(F32)
            copy(out=words[:, half * COLS:(half + 1) * COLS].rearrange("p (d n u) -> p d n u", d=2, u=2),
                 in_=turned[c, half][:].rearrange("p d u n -> p d n u"))

        def quantize(c):
            codes[c] = work.tile([P, COLS], U32, name="codes", bufs=4, align_bytes=64)
            scales[c] = work.tile([P, COLS], U8, name="scales", bufs=4, align_bytes=64)
            nc.vector.quantize_mx(out=codes[c][:].bitcast(FP8X4), scales=scales[c][:], in_=q_in[c][:])

        def layer(c):
            for o in range(2):
                if c >= Z_IN_TR:
                    z[c, o] = ps.tile([P, COLS], F32, name="tr", bufs=3)
                else:
                    z[c, o] = ps.tile([P, COLS], F32, name="z", bufs=2)
                nc.tensor.matmul_mx(
                    out=z[c, o][:],
                    lhsT=w_codes[:, o * P:(o + 1) * P].bitcast(FP8X4), lhsT_scale=w_scales[:, o * P:(o + 1) * P],
                    rhs=codes[c][:].bitcast(FP8X4), rhs_scale=scales[c][:], start=True, stop=True)

        def relu(c, o):
            if o == 0:
                y[c] = work.tile([P, 2, COLS], F32, name="y", bufs=4)
            if (c, o) not in ON_VECTOR:
                w = COLS // 2 if (c, o) in PAIRED else COLS
                nc.scalar.activation(
                    out=y[c][:, o, 0:w], in_=z[c, o][:, 0:w], func=ACT.Relu, bias=b3_col[:, o:o + 1])

        def relu_on_vector(c, o):
            neg_b = neg_b3_col[:, o:o + 1]
            t = c // PER_NT
            if (c, o) in ON_VECTOR:
                if (t, o) not in sums:
                    sums[t, o] = work.tile([P, COLS], F32, name="sums", bufs=4)
                    nc.vector.tensor_scalar(
                        out=sums[t, o][:], in0=z[c, o][:], scalar1=neg_b, scalar2=None, op0=ALU.max)
                else:
                    nc.vector.scalar_tensor_tensor(
                        out=sums[t, o][:], in0=z[c, o][:], scalar=neg_b, in1=sums[t, o][:],
                        op0=ALU.max, op1=ALU.add)
            if (c, o) in PAIRED:
                w = COLS // 2
                nc.vector.scalar_tensor_tensor(
                    out=y[c][:, o, w:COLS], in0=z[c, o][:, w:COLS], scalar=neg_b, in1=y[c][:, o, 0:w],
                    op0=ALU.max, op1=ALU.add)

        def pool(c):
            t, last = c // PER_NT, c % PER_NT == PER_NT - 1
            if c % PER_NT == 0:
                pooled_ps[t] = ps.tile([P, FINAL], F32, name="pooled_ps", bufs=1)
            blocks = []
            for o in range(2):
                if last and (t, o) in sums:
                    blocks.extend([(o, sums[t, o][:, i * P:(i + 1) * P]) for i in range(CD)])
            for o in range(2):
                if (c, o) not in ON_VECTOR:
                    first = CD // 2 if (c, o) in PAIRED else 0
                    blocks.extend([(o, y[c][:, o, i * P:(i + 1) * P]) for i in range(first, CD)])
            for i, (o, data) in enumerate(blocks):
                add_transpose(pooled_ps[t][:, 2 * G + o * P:2 * G + (o + 1) * P], data,
                              start=(c % PER_NT == 0 and i == 0), stop=(last and i == len(blocks) - 1))

        plain_ps = {}
        plain_sb = {}
        rest_ps = {}
        rest_sb = {}
        pair_sums = {}

        def x_plain(t, i):
            if i == 0:
                plain_ps[t] = ps.tile([P, 2 * G, 2], F32, name="plain_ps", bufs=1)
            nc.tensor.matmul(plain_ps[t][:], lhsT=ident_b[:], rhs=x12_sb[t][:, :, 2 * i:2 * i + 2],
                             start=(i == 0), stop=(i == PLAIN_D // 2 - 1))

        def x_plain_out(t):
            plain_sb[t] = work.tile([P, 2 * G], F32, name="plain_sb", bufs=2)
            nc.vector.tensor_reduce(
                out=plain_sb[t][:], in_=plain_ps[t][:], axis=mybir.AxisListType.X, op=ALU.add)

        def x_pairs(t, k):
            if k == 0:
                pair_sums[t] = work.tile([P, PAIRS, 2 * G], F32, name="pair_sums", bufs=2)
            i0, n, c0, c1 = PIECES[k]
            d0 = PLAIN_D + i0
            nc.vector.tensor_tensor(
                out=pair_sums[t][:, i0:i0 + n, c0:c1].rearrange("n i c -> n c i"),
                in0=x12_sb[t][:, c0:c1, d0:d0 + n], in1=x12_sb[t][:, c0:c1, d0 + PAIRS:d0 + PAIRS + n], op=ALU.add)

        def x_rest(t, k):
            i0, n, c0, c1 = PIECES[k]
            if k == 0:
                rest_ps[t] = ps.tile([P, 2, P], F32, name="rest_ps", bufs=1)
            for o in range(c0 // G, c1 // G):
                for i in range(i0, i0 + n):
                    add_transpose(rest_ps[t][:, o, :], pair_sums[t][:, i, o * P:(o + 1) * P],
                                  start=(o == 0 and i == 0), stop=(o == 1 and i == PAIRS - 1))

        def x_rest_out(t):
            rest_sb[t] = work.tile([P, 2, P], F32, name="rest_sb", bufs=2)
            nc.scalar.copy(out=rest_sb[t][:], in_=rest_ps[t][:])

        def x_rest_back(t):
            for o in range(2):
                add_transpose(pooled_ps[t][:, o * P:(o + 1) * P], rest_sb[t][:, o, :], start=False, stop=False)

        pooled = {}
        pooled_turned = {}
        pooled_q = {}
        pooled_codes = {}
        pooled_scales = {}
        out_ps = {}

        def finish_pooled(t):
            pooled[t] = work.tile([P, FINAL], BF16, name="pooled", bufs=2)
            nc.vector.tensor_tensor(
                out=pooled[t][:, 0:2 * G], in0=pooled_ps[t][:, 0:2 * G], in1=plain_sb[t][:], op=ALU.add)
            for o in range(2):
                missing = sum([CD // 2 for c, half in PAIRED if c // PER_NT == t and half == o])
                missing = missing + sum([CD for c, half in ON_VECTOR if c // PER_NT == t and half == o])
                cols = slice(2 * G + o * P, 2 * G + (o + 1) * P)
                if missing:
                    nc.vector.scalar_tensor_tensor(
                        out=pooled[t][:, cols], in0=b3_row[:, o * P:(o + 1) * P], scalar=float(missing),
                        in1=pooled_ps[t][:, cols], op0=ALU.mult, op1=ALU.add)
                else:
                    nc.scalar.copy(out=pooled[t][:, cols], in_=pooled_ps[t][:, cols])

        def finish_transpose(t):
            words = pooled[t][:].bitcast(F32)
            pooled_turned[t] = ps.tile([P, 2, P], F32, name="tr", bufs=3)
            for u in range(2):
                nc.tensor.transpose(pooled_turned[t][:, u, :], words[:, u:FINAL // 2:2], ident_f[:])

        def finish_unload(t):
            pooled_q[t] = work.tile([P, 4 * P], BF16, name="pooled_q", bufs=2, align_bytes=64)
            nc.scalar.copy(out=pooled_q[t][:].bitcast(F32).rearrange("p (n u) -> p n u", u=2),
                           in_=pooled_turned[t][:].rearrange("p u n -> p n u"))

        def finish_quantize(t):
            pooled_codes[t] = work.tile([P, P], U32, name="pooled_codes", bufs=2, align_bytes=64)
            pooled_scales[t] = work.tile([P, P], U8, name="pooled_scales", bufs=2, align_bytes=64)
            nc.vector.quantize_mx(
                out=pooled_codes[t][:].bitcast(FP8X4), scales=pooled_scales[t][:], in_=pooled_q[t][:])

        def finish_matmul(t):
            out_ps[t] = ps.tile([P, NOUT], F32, name="tr", bufs=3)
            nc.tensor.matmul_mx(
                out=out_ps[t][:], lhsT=pooled_codes[t][:].bitcast(FP8X4), lhsT_scale=pooled_scales[t][:],
                rhs=ow_codes[:].bitcast(FP8X4), rhs_scale=ow_scales[:], start=True, stop=True)

        def finish_store(t):
            result = work.tile([P, NOUT], F32, name="result", bufs=2)
            nc.vector.tensor_tensor(out=result[:], in0=out_ps[t][:], in1=ob_row[:], op=ALU.add)
            nc.sync.dma_start(out=out[t * P:(t + 1) * P, :], in_=result[:])

        def prepare_out_w():
            for j in range(4):
                nc.vector.tensor_scalar(
                    out=ow_q[:, :, j], in0=ow_raw[:, j * NOUT:(j + 1) * NOUT].bitcast(FP8),
                    scalar1=ow_scale[:, j:j + 1], scalar2=None, op0=ALU.mult)
            nc.vector.quantize_mx(out=ow_codes[:].bitcast(FP8X4), scales=ow_scales[:],
                                  in_=ow_q[:].rearrange("p n j -> p (n j)"))

        arrange(0, nc.vector.tensor_copy, 0, G // 2)
        pair_x()
        arrange(0, nc.vector.tensor_copy, G // 2, G)
        arrange(1, nc.scalar.copy)
        for f in range(F):
            product(0, f)
        transpose_chunk(0)
        arrange(2, nc.scalar.copy)
        arrange(3, nc.scalar.copy)
        unload(0, 0, nc.scalar.copy)
        unload(0, 1, nc.scalar.copy)
        for f in range(F):
            product(1, f)

        for u in range(2):
            nc.vector.tensor_copy(out=w_perm[:, :, u, :, :],
                                  in_=w_raw[:].rearrange("o h (q u w) -> o u h q w", u=2, w=16)[:, u])
        b3_ps = ps.tile([P, 2, P], BF16, name="rest_ps", bufs=1)
        for o in range(2):
            nc.tensor.transpose(b3_ps[:, o, :], b3_row[:, o * P:(o + 1) * P], ident_b[:])
        w_turned = ps.tile([P, 2, 2, P], F32, name="tr", bufs=3)
        w_words = w_perm[:].rearrange("o h u q w -> o (h u q w)").bitcast(F32)
        for o in range(2):
            for u in range(2):
                nc.tensor.transpose(
                    w_turned[:, o, u, :], w_words[:, (2 * o + u) * P:(2 * o + u + 1) * P], ident_f[:])
        nc.scalar.copy(out=w_q[:].bitcast(F32).rearrange("p (h o u) -> p h o u", h=2, u=2),
                       in_=w_turned[:].rearrange("p h u o -> p h o u"))
        nc.scalar.copy(out=b3_col[:], in_=b3_ps[:, :, 0])
        for f in range(F):
            product(2, f)
            if f == 1:
                quantize(0)
        nc.vector.quantize_mx(out=w_codes[:].bitcast(FP8X4), scales=w_scales[:], in_=w_q[:])
        arrange(4, nc.scalar.copy)
        for c in range(5, ARRANGE_AHEAD + 1):
            arrange(c, nc.vector.tensor_copy)

        for s in range(1, CHUNKS + 6):
            tiles = [(t, s - PER_NT * t, FINISH_LAST if t == NT - 1 else FINISH) for t in range(NT)]
            c_relu = s - RELU if 0 <= s - RELU < CHUNKS else None

            for t, at, finish in tiles:
                if at == finish[0]:
                    finish_pooled(t)
            if c_relu is not None:
                relu(c_relu, 0)
            if s < CHUNKS:
                transpose_chunk(s)
                unload(s, 0, nc.scalar.copy)
            if c_relu is not None:
                relu(c_relu, 1)
            if s < CHUNKS - 1:
                unload(s, 1, nc.scalar.copy)
            for t, at, finish in tiles:
                if at == X_REST_OUT[t]:
                    x_rest_out(t)
            if s == X12_STEP:
                load_x12(NT - 1)

            for t, at, finish in tiles:
                if at == finish[4] + 1 and t < NT - 1:
                    finish_store(t)
            for step, r, f in PRODUCTS:
                if step == s:
                    product(r, f)
            if 1 <= s - QUANTIZE < CHUNKS:
                quantize(s - QUANTIZE)
            if s == CHUNKS - 1:
                unload(s, 1, nc.vector.tensor_copy)
            if c_relu is not None:
                relu_on_vector(c_relu, 0)
                relu_on_vector(c_relu, 1)
            if s + ARRANGE_AHEAD < CHUNKS:
                arrange(s + ARRANGE_AHEAD, nc.vector.tensor_copy)
            for t, at, finish in tiles:
                for k in range(len(PIECES)):
                    if at == X_PAIRS[t][k]:
                        x_pairs(t, k)
                if at == X_PLAIN_OUT[t]:
                    x_plain_out(t)
                if at == finish[3]:
                    finish_quantize(t)
            if s == LAYER:
                nc.vector.tensor_scalar(
                    out=neg_b3_col[:], in0=b3_col[:], scalar1=-1.0, scalar2=None, op0=ALU.mult)
            if s == OUT_W_STEP:
                prepare_out_w()

            for t, at, finish in tiles:
                if at == finish[1]:
                    finish_transpose(t)
                if at == X_REST_BACK[t]:
                    x_rest_back(t)
            if CHUNKS <= s < CHUNKS + LAYER:
                layer(s - LAYER)
            if 0 <= s - POOL < CHUNKS:
                pool(s - POOL)
            for t, at, finish in tiles:
                for k in range(len(PIECES)):
                    if at == X_REST[t][k]:
                        x_rest(t, k)
            for t, at, finish in tiles:
                for i in range(PLAIN_D // 2):
                    if at == X_PLAIN[t][i]:
                        x_plain(t, i)
            if LAYER <= s < CHUNKS:
                layer(s - LAYER)
            for t, at, finish in tiles:
                if at == finish[2]:
                    finish_unload(t)
                if at == finish[4]:
                    finish_matmul(t)
                    if t == NT - 1:
                        finish_store(t)
